import numpy as np
import ml_dtypes


def mxq(x, axis, fmt="e4m3"):
    dtype, down = {"e4m3": (ml_dtypes.float8_e4m3fn, 7), "e5m2": (ml_dtypes.float8_e5m2, 14)}[fmt]
    v = np.moveaxis(np.asarray(x, np.float32).astype(ml_dtypes.bfloat16).astype(np.float64), axis, -1)
    blocks = v.reshape(v.shape[:-1] + (-1, 32))
    amax = np.abs(blocks).max(-1, keepdims=True)
    byte = np.maximum(np.where(amax > 0, np.frexp(amax)[1] - 1 + 127, 0) - down, 1)
    scale = np.exp2(byte - 127.0)
    codes = (blocks / scale).astype(np.float32).astype(dtype).astype(np.float64)
    return np.moveaxis((codes * scale).reshape(v.shape), -1, axis)


WIDE = False


def mx_kscale(k):
    if not WIDE:
        return np.ones(k)
    levels = np.array([10, -10, 5, -5, 0])
    a = np.random.permutation(np.resize(levels, k // 512 * 4)).reshape(k // 512, 4)
    idx = np.arange(k)
    return np.exp2(a[idx // 512, idx % 128 // 32])


BF16 = ml_dtypes.bfloat16


def bf(x):
    return np.asarray(x, np.float32).astype(BF16)


def f64(x):
    return np.asarray(x).astype(np.float64)


E2M1 = np.array([0.0, 0.5, 1.0, 1.5, 2.0, 3.0, 4.0, 6.0, -0.0, -0.5, -1.0, -1.5, -2.0, -3.0, -4.0, -6.0])


def pack_weight(w, fmt):
    k, n = w.shape
    w = f64(bf(w)).reshape(k // 32, 32, n)
    amax = np.abs(w).max(1)
    if fmt == "e4m3":
        byte = np.frexp(amax)[1] - 1 + 127 - 7
    else:
        mant, ex = np.frexp(amax / 6.0)
        byte = np.where(mant > 0.5, ex, ex - 1) + 127
    byte = np.clip(np.where(amax > 0, byte, 1), 1, 254)
    scaled = (w * np.exp2(127.0 - byte)[:, None, :]).reshape(k, n).astype(np.float32)
    by_word = np.ascontiguousarray(scaled.reshape(k // 512, 128, 4, n).transpose(0, 1, 3, 2))
    if fmt == "e4m3":
        words = by_word.astype(ml_dtypes.float8_e4m3fn).view(np.uint8)
    else:
        c = by_word.astype(ml_dtypes.float4_e2m1fn).view(np.uint8) & 0xF
        words = c[..., 0::2] | (c[..., 1::2] << 4)
    return np.ascontiguousarray(words), np.ascontiguousarray(byte.astype(np.uint8).reshape(k // 512, 16, n))


def unpack_weight(words, scales, fmt):
    g, p, n, _ = words.shape
    if fmt == "e4m3":
        vals = np.ascontiguousarray(words).view(ml_dtypes.float8_e4m3fn).astype(np.float64)
    else:
        nib = np.empty((g, p, n, 4), np.uint8)
        nib[..., 0::2] = words & 0xF
        nib[..., 1::2] = words >> 4
        vals = E2M1[nib]
    vals = vals * np.repeat(np.exp2(scales.astype(np.float64) - 127.0), 8, axis=1)[..., None]
    return vals.transpose(0, 1, 3, 2).reshape(g * 512, n)


B, S, FIN, D, AF, F, H = 4, 1024, 128, 512, 2048, 1024, 16
EPS = 1e-3
FMT = "e4m3"


def layer_norm(v, gamma, beta):
    mu = v.mean(-1, keepdims=True)
    var = v.var(-1, keepdims=True)
    return (v - mu) / np.sqrt(var + EPS) * gamma + beta


def setup_inputs():
    r = np.random.standard_normal
    t = mx_kscale(F)
    h_attn = bf(r((B, S, D)))
    W1_words, W1_scales = pack_weight(r((D, F)) / np.sqrt(D) * t, FMT)
    b1 = bf(0.1 * r(F) * t)
    W2_words, W2_scales = pack_weight(r((F, D)) / np.sqrt(F) / t[:, None], FMT)
    b2 = bf(0.1 * r(D))
    g2 = bf(1.0 + 0.1 * r(D))
    beta2 = bf(0.1 * r(D))
    return {"h_attn": h_attn,
            "W1_words": W1_words, "W1_scales": W1_scales, "b1": b1,
            "W2_words": W2_words, "W2_scales": W2_scales, "b2": b2,
            "g2": g2, "beta2": beta2}


def reference(h_attn, W1_words, W1_scales, b1, W2_words, W2_scales, b2, g2, beta2):
    h = f64(h_attn)
    hid = np.maximum((mxq(h, 2, "e4m3") @ unpack_weight(W1_words, W1_scales, FMT)) + f64(b1), 0.0)
    ffn = (mxq(hid, 2, "e4m3") @ unpack_weight(W2_words, W2_scales, FMT)) + f64(b2)
    return layer_norm(h + ffn, f64(g2), f64(beta2))

@@ -1,0 +1,236 @@
+from contextlib import ExitStack
+
+import concourse.mybir as mybir
+from concourse.masks import make_identity
+
+F32 = mybir.dt.float32
+BF16 = mybir.dt.bfloat16
+I32 = mybir.dt.int32
+U32 = mybir.dt.uint32
+U8 = mybir.dt.uint8
+FP8X4 = mybir.dt.float8_e4m3fn_x4
+ALU = mybir.AluOpType
+FUNC = mybir.ActivationFunctionType
+
+P = 128
+TOKENS = 4096
+D = 512
+F = 1024
+K_PASS = 512
+F_PASSES = F // K_PASS
+TILES = TOKENS // P
+ROUND = 4
+ROUNDS = TILES // ROUND
+EPS = 1e-3
+
+FLOPS = 2 * TOKENS * D * F * 2
+
+
+def tile_ffnn_encoder_pc_t_kernel(
+    tc, h_attn, W1_words, W1_scales, b1, W2_words, W2_scales, b2, g2, beta2, out
+):
+    nc = tc.nc
+    h_rows = h_attn.flatten_outer_dims().rearrange("(p n) d -> p n d", p=P)
+    out_rows = out.flatten_outer_dims().rearrange("(p n) d -> p n d", p=P)
+
+    with ExitStack() as ctx:
+        const = ctx.enter_context(tc.tile_pool(name="const", bufs=1))
+        work = ctx.enter_context(tc.tile_pool(name="work", bufs=2))
+        psum = ctx.enter_context(tc.psum_pool(name="psum", bufs=2))
+
+        h_sb = const.tile([P, TILES, D], BF16)
+        w1_codes = const.tile([P, F], U32, align_bytes=64)
+        w1_plane = const.tile([P, F], U8, align_bytes=64)
+        w2_codes = const.tile([P, F_PASSES, D], U32, align_bytes=64)
+        w2_plane = const.tile([P, F_PASSES, D], U8, align_bytes=64)
+        vec_rows = const.tile([P, F + 3 * D], BF16)
+        spread = const.tile([P, F + 3 * D], F32)
+        ones = const.tile([P, P], BF16)
+        ident = const.tile([P, P], F32)
+        one_col = const.tile([P, 1], F32)
+        sqrt_warm = const.tile([P, 1], F32)
+
+        nc.vector.memset(w1_plane[:].bitcast(I32), 0)
+        nc.vector.memset(w2_plane[:].bitcast(I32), 0)
+        nc.vector.memset(vec_rows[:].bitcast(I32), 0)
+        nc.vector.memset(ones[:], 1.0)
+        nc.vector.memset(one_col[:], 1.0)
+        make_identity(nc, ident[:])
+        nc.scalar.activation(out=sqrt_warm[:], in_=one_col[:], func=FUNC.Sqrt)
+
+        def load_h(r):
+            tiles = slice(r * ROUND, (r + 1) * ROUND)
+            nc.sync.dma_start(out=h_sb[:, tiles, :], in_=h_rows[:, tiles, :])
+
+        load_h(0)
+        nc.sync.dma_start(out=vec_rows[0:1, 0:F], in_=b1.rearrange("(o n) -> o n", o=1))
+        for row in range(4):
+            nc.sync.dma_start(
+                out=w1_plane[row:P:32, :].bitcast(I32),
+                in_=W1_scales[0, row:16:4, :].bitcast(I32),
+            )
+        nc.sync.dma_start(
+            out=w1_codes[:].bitcast(I32),
+            in_=W1_words[0].rearrange("p n t -> p (n t)").bitcast(I32),
+        )
+        load_h(1)
+        for i, vec in enumerate((b2, g2, beta2)):
+            nc.sync.dma_start(
+                out=vec_rows[0:1, F + i * D : F + (i + 1) * D],
+                in_=vec.rearrange("(o n) -> o n", o=1),
+            )
+        for g in range(F_PASSES):
+            for row in range(4):
+                nc.sync.dma_start(
+                    out=w2_plane[row:P:32, g, :].bitcast(I32),
+                    in_=W2_scales[g, row:16:4, :].bitcast(I32),
+                )
+        for g in range(F_PASSES):
+            nc.sync.dma_start(
+                out=w2_codes[:, g, :].bitcast(I32),
+                in_=W2_words[g].rearrange("p n t -> p (n t)").bitcast(I32),
+            )
+        for r in range(2, ROUNDS):
+            load_h(r)
+
+        for c in range(F // 512 + 3):
+            cols = slice(c * 512, (c + 1) * 512)
+            bank = psum.tile([P, 512], F32, tag="acc1", bufs=3)
+            nc.tensor.matmul(out=bank[:], lhsT=ones[:], rhs=vec_rows[:, cols], start=True, stop=True)
+            if c < F // 512:
+                nc.scalar.copy(
+                    out=spread[:, cols].rearrange("k (u p e) -> k u p e", u=2, e=2),
+                    in_=bank[:].rearrange("k (p u e) -> k u p e", u=2, e=2),
+                )
+            else:
+                nc.scalar.copy(out=spread[:, cols], in_=bank[:])
+        b1_sorted = spread[:, 0:F]
+        b2_all = spread[:, F : F + D]
+        g2_all = spread[:, F + D : F + 2 * D]
+        beta2_all = spread[:, F + 2 * D : F + 3 * D]
+
+        def quantise_h(r):
+            h_grouped = work.tile([P, ROUND * P * 4], BF16, align_bytes=64, tag="h_grouped")
+            for half in range(ROUND // 2):
+                hT = psum.tile([P, 2, 2, P], F32, tag="hT", bufs=1)
+                for j in range(2):
+                    words = h_sb[:, r * ROUND + half * 2 + j, :].bitcast(F32)
+                    for u in range(2):
+                        nc.tensor.transpose(hT[:, j, u, :], words[:, u : D // 2 : 2], ident[:])
+                nc.scalar.copy(
+                    out=h_grouped[:, half * 2 * P * 4 : (half + 1) * 2 * P * 4]
+                    .bitcast(F32)
+                    .rearrange("p (j k u) -> p j k u", j=2, u=2),
+                    in_=hT[:].rearrange("p j u k -> p j k u"),
+                )
+            hq_codes = work.tile([P, ROUND * P], U32, align_bytes=64, tag="hq_codes")
+            hq_plane = work.tile([P, ROUND * P], U8, align_bytes=64, tag="hq_plane")
+            nc.vector.quantize_mx(out=hq_codes[:].bitcast(FP8X4), scales=hq_plane[:], in_=h_grouped[:])
+            return hq_codes, hq_plane
+
+        def hidden(hq_codes, hq_plane):
+            hid_codes = work.tile([P, ROUND, F_PASSES, P], U32, align_bytes=64, tag="hid_codes")
+            hid_plane = work.tile([P, ROUND, F_PASSES, P], U8, align_bytes=64, tag="hid_plane")
+            for pair in range(ROUND // 2):
+                hid_grouped = work.tile([P, 2, F_PASSES, P * 4], BF16, align_bytes=64, tag="hid_grouped")
+                for jj in range(2):
+                    j = pair * 2 + jj
+                    toks = slice(j * P, (j + 1) * P)
+                    hid_sorted = work.tile([P, F_PASSES, K_PASS], BF16, tag="hid_sorted", bufs=4)
+                    for g in range(F_PASSES):
+                        cols = slice(g * K_PASS, (g + 1) * K_PASS)
+                        acc1 = psum.tile([P, 512], F32, tag="acc1", bufs=3)
+                        nc.tensor.matmul_mx(
+                            out=acc1[:],
+                            lhsT=hq_codes[:, toks].bitcast(FP8X4),
+                            lhsT_scale=hq_plane[:, toks],
+                            rhs=w1_codes[:, cols].bitcast(FP8X4),
+                            rhs_scale=w1_plane[:, cols],
+                            start=True,
+                            stop=True,
+                        )
+                        nc.vector.tensor_tensor(
+                            out=hid_sorted[:, g, :].rearrange("k (u p e) -> k u p e", u=2, e=2),
+                            in0=acc1[:].rearrange("k (p u e) -> k u p e", u=2, e=2),
+                            in1=b1_sorted[:, cols].rearrange("k (u p e) -> k u p e", u=2, e=2),
+                            op=ALU.add,
+                        )
+                    hidT = psum.tile([P, F_PASSES, 2, P], F32, tag="hidT", bufs=2)
+                    for g in range(F_PASSES):
+                        words = hid_sorted[:, g, :].bitcast(F32)
+                        for u in range(2):
+                            nc.tensor.transpose(hidT[:, g, u, :], words[:, u * P : (u + 1) * P], ident[:])
+                    for g in range(F_PASSES):
+                        nc.scalar.activation(
+                            out=hid_grouped[:, jj, g, :].rearrange("p (k u e) -> p k u e", u=2, e=2),
+                            in_=hidT[:, g, :, :].bitcast(BF16).rearrange("p u (k e) -> p k u e", e=2),
+                            func=FUNC.Relu,
+                        )
+                nc.vector.quantize_mx(
+                    out=hid_codes[:, pair * 2 : pair * 2 + 2, :, :]
+                    .rearrange("p j g k -> p (j g k)")
+                    .bitcast(FP8X4),
+                    scales=hid_plane[:, pair * 2 : pair * 2 + 2, :, :].rearrange("p j g k -> p (j g k)"),
+                    in_=hid_grouped[:].rearrange("p j g c -> p (j g c)"),
+                )
+            return hid_codes, hid_plane
+
+        def residual_plus_b2(r):
+            hb = work.tile([P, ROUND, D], F32, tag="hb", bufs=3)
+            for j in range(ROUND):
+                nc.gpsimd.tensor_tensor(out=hb[:, j, :], in0=h_sb[:, r * ROUND + j, :], in1=b2_all, op=ALU.add)
+            return hb
+
+        def output(r, hid_codes, hid_plane, hb):
+            resid = work.tile([P, ROUND, D], F32, tag="resid")
+            sums = work.tile([P, ROUND], F32, tag="sums")
+            neg_mean = work.tile([P, ROUND], F32, tag="neg_mean")
+            sq_sums = work.tile([P, ROUND], F32, tag="sq_sums")
+            std = work.tile([P, ROUND], F32, tag="std")
+            rstd = work.tile([P, ROUND], F32, tag="rstd")
+            for j in range(ROUND):
+                acc2 = psum.tile([P, D], F32, tag="acc2", bufs=2)
+                for g in range(F_PASSES):
+                    nc.tensor.matmul_mx(
+                        out=acc2[:],
+                        lhsT=hid_codes[:, j, g, :].bitcast(FP8X4),
+                        lhsT_scale=hid_plane[:, j, g, :],
+                        rhs=w2_codes[:, g, :].bitcast(FP8X4),
+                        rhs_scale=w2_plane[:, g, :],
+                        start=(g == 0),
+                        stop=(g == F_PASSES - 1),
+                    )
+                nc.vector.scalar_tensor_tensor(
+                    out=resid[:, j, :], in0=acc2[:], scalar=1.0, in1=hb[:, j, :],
+                    op0=ALU.mult, op1=ALU.add, accum_out=sums[:, j : j + 1],
+                )
+            nc.vector.tensor_scalar_mul(out=neg_mean[:], in0=sums[:], scalar1=-1.0 / D)
+            for j in range(ROUND):
+                squares = work.tile([P, D], BF16, tag="squares")
+                nc.scalar.activation(
+                    out=squares[:], in_=resid[:, j, :], func=FUNC.Square,
+                    bias=neg_mean[:, j : j + 1], scale=1.0, accum_out=sq_sums[:, j : j + 1],
+                )
+            nc.scalar.activation(out=std[:], in_=sq_sums[:], func=FUNC.Sqrt, bias=EPS, scale=1.0 / D)
+            nc.vector.reciprocal(out=rstd[:], in_=std[:])
+            for j in range(ROUND):
+                scaled = work.tile([P, D], F32, tag="scaled", bufs=3)
+                nc.vector.scalar_tensor_tensor(
+                    out=scaled[:], in0=resid[:, j, :], scalar=neg_mean[:, j : j + 1], in1=g2_all,
+                    op0=ALU.add, op1=ALU.mult,
+                )
+                normed = work.tile([P, D], F32, tag="normed", bufs=4)
+                nc.vector.scalar_tensor_tensor(
+                    out=normed[:], in0=scaled[:], scalar=rstd[:, j : j + 1], in1=beta2_all,
+                    op0=ALU.mult, op1=ALU.add,
+                )
+                nc.sync.dma_start(out=out_rows[:, r * ROUND + j, :], in_=normed[:])
+
+        quantised_h = quantise_h(0)
+        for r in range(ROUNDS):
+            this_h = quantised_h
+            if r + 1 < ROUNDS:
+                quantised_h = quantise_h(r + 1)
+            hb = residual_plus_b2(r)
+            hid_codes, hid_plane = hidden(this_h[0], this_h[1])
+            output(r, hid_codes, hid_plane, hb)

@@ -18,8 +18,10 @@ D = 512
 F = 1024
 K_PASS = 512
 F_PASSES = F // K_PASS
+F_CHUNKS = F // P
 TILES = TOKENS // P
 ROUND = 4
+ROUND_TOKENS = ROUND * P
 ROUNDS = TILES // ROUND
 EPS = 1e-3
 
@@ -36,26 +38,32 @@ def tile_ffnn_encoder_pc_t_kernel(
     with ExitStack() as ctx:
         const = ctx.enter_context(tc.tile_pool(name="const", bufs=1))
         work = ctx.enter_context(tc.tile_pool(name="work", bufs=2))
-        psum = ctx.enter_context(tc.psum_pool(name="psum", bufs=2))
+        psum = ctx.enter_context(tc.psum_pool(name="psum", bufs=8))
 
         h_sb = const.tile([P, TILES, D], BF16)
+        hb_sb = const.tile([P, TILES, D], F32)
         w1_codes = const.tile([P, F], U32, align_bytes=64)
         w1_plane = const.tile([P, F], U8, align_bytes=64)
         w2_codes = const.tile([P, F_PASSES, D], U32, align_bytes=64)
         w2_plane = const.tile([P, F_PASSES, D], U8, align_bytes=64)
-        vec_rows = const.tile([P, F + 3 * D], BF16)
-        spread = const.tile([P, F + 3 * D], F32)
+        b1_rows = const.tile([P, P], BF16)
+        b1_col = const.tile([P, F_CHUNKS], F32)
+        vec_rows = const.tile([P, 3 * D], BF16)
+        spread = const.tile([P, 3 * D], F32)
         ones = const.tile([P, P], BF16)
         ident = const.tile([P, P], F32)
+        ident_bf = const.tile([P, P], BF16)
         one_col = const.tile([P, 1], F32)
         sqrt_warm = const.tile([P, 1], F32)
 
+        nc.vector.memset(b1_rows[:].bitcast(I32), 0)
+        nc.vector.memset(vec_rows[:].bitcast(I32), 0)
         nc.vector.memset(w1_plane[:].bitcast(I32), 0)
         nc.vector.memset(w2_plane[:].bitcast(I32), 0)
-        nc.vector.memset(vec_rows[:].bitcast(I32), 0)
         nc.vector.memset(ones[:], 1.0)
         nc.vector.memset(one_col[:], 1.0)
         make_identity(nc, ident[:])
+        make_identity(nc, ident_bf[:])
         nc.scalar.activation(out=sqrt_warm[:], in_=one_col[:], func=FUNC.Sqrt)
 
         def load_h(r):
@@ -63,7 +71,11 @@ def tile_ffnn_encoder_pc_t_kernel(
             nc.sync.dma_start(out=h_sb[:, tiles, :], in_=h_rows[:, tiles, :])
 
         load_h(0)
-        nc.sync.dma_start(out=vec_rows[0:1, 0:F], in_=b1.rearrange("(o n) -> o n", o=1))
+        nc.sync.dma_start(out=b1_rows[0:F_CHUNKS, :], in_=b1.rearrange("(j m) -> j m", m=P))
+        for i, vec in enumerate((b2, g2, beta2)):
+            nc.sync.dma_start(
+                out=vec_rows[0:1, i * D : (i + 1) * D], in_=vec.rearrange("(o n) -> o n", o=1)
+            )
         for row in range(4):
             nc.sync.dma_start(
                 out=w1_plane[row:P:32, :].bitcast(I32),
@@ -74,11 +86,6 @@ def tile_ffnn_encoder_pc_t_kernel(
             in_=W1_words[0].rearrange("p n t -> p (n t)").bitcast(I32),
         )
         load_h(1)
-        for i, vec in enumerate((b2, g2, beta2)):
-            nc.sync.dma_start(
-                out=vec_rows[0:1, F + i * D : F + (i + 1) * D],
-                in_=vec.rearrange("(o n) -> o n", o=1),
-            )
         for g in range(F_PASSES):
             for row in range(4):
                 nc.sync.dma_start(
@@ -93,144 +100,202 @@ def tile_ffnn_encoder_pc_t_kernel(
         for r in range(2, ROUNDS):
             load_h(r)
 
-        for c in range(F // 512 + 3):
-            cols = slice(c * 512, (c + 1) * 512)
-            bank = psum.tile([P, 512], F32, tag="acc1", bufs=3)
-            nc.tensor.matmul(out=bank[:], lhsT=ones[:], rhs=vec_rows[:, cols], start=True, stop=True)
-            if c < F // 512:
-                nc.scalar.copy(
-                    out=spread[:, cols].rearrange("k (u p e) -> k u p e", u=2, e=2),
-                    in_=bank[:].rearrange("k (p u e) -> k u p e", u=2, e=2),
-                )
-            else:
-                nc.scalar.copy(out=spread[:, cols], in_=bank[:])
-        b1_sorted = spread[:, 0:F]
-        b2_all = spread[:, F : F + D]
-        g2_all = spread[:, F + D : F + 2 * D]
-        beta2_all = spread[:, F + 2 * D : F + 3 * D]
+        b2_all = spread[:, 0:D]
+        g2_all = spread[:, D : 2 * D]
+        beta2_all = spread[:, 2 * D : 3 * D]
 
-        def quantise_h(r):
-            h_grouped = work.tile([P, ROUND * P * 4], BF16, align_bytes=64, tag="h_grouped")
+        def prepare_vectors():
+            flipped = psum.tile([P, F], BF16, tag="bank")
+            nc.tensor.transpose(flipped[:, 0:P], b1_rows[:], ident_bf[:])
+            nc.vector.tensor_copy(out=b1_col[:], in_=flipped[:, 0:F_CHUNKS])
+            for i in range(3):
+                cols = slice(i * D, (i + 1) * D)
+                bank = psum.tile([P, D], F32, tag="bank")
+                nc.tensor.matmul(out=bank[:], lhsT=ones[:], rhs=vec_rows[:, cols], start=True, stop=True)
+                nc.vector.tensor_copy(out=spread[:, cols], in_=bank[:])
+            for n in range(TILES):
+                nc.gpsimd.tensor_tensor(out=hb_sb[:, n, :], in0=h_sb[:, n, :], in1=b2_all, op=ALU.add)
+
+        h_grouped = {}
+        hq = {}
+        hid_by_unit = {}
+        hid_sorted = {}
+        hid_grouped = {}
+        hidq = {}
+        resid = {}
+        stats = {}
+        scaled = {}
+
+        def transpose_h(r):
+            grouped = work.tile([P, ROUND_TOKENS * 4], BF16, align_bytes=64, tag="h_grouped")
+            h_grouped[r] = grouped
             for half in range(ROUND // 2):
-                hT = psum.tile([P, 2, 2, P], F32, tag="hT", bufs=1)
+                hT = psum.tile([P, 2, 2, P], F32, tag="bank")
                 for j in range(2):
                     words = h_sb[:, r * ROUND + half * 2 + j, :].bitcast(F32)
                     for u in range(2):
                         nc.tensor.transpose(hT[:, j, u, :], words[:, u : D // 2 : 2], ident[:])
                 nc.scalar.copy(
-                    out=h_grouped[:, half * 2 * P * 4 : (half + 1) * 2 * P * 4]
+                    out=grouped[:, half * 2 * P * 4 : (half + 1) * 2 * P * 4]
                     .bitcast(F32)
                     .rearrange("p (j k u) -> p j k u", j=2, u=2),
                     in_=hT[:].rearrange("p j u k -> p j k u"),
                 )
-            hq_codes = work.tile([P, ROUND * P], U32, align_bytes=64, tag="hq_codes")
-            hq_plane = work.tile([P, ROUND * P], U8, align_bytes=64, tag="hq_plane")
-            nc.vector.quantize_mx(out=hq_codes[:].bitcast(FP8X4), scales=hq_plane[:], in_=h_grouped[:])
-            return hq_codes, hq_plane
 
-        def hidden(hq_codes, hq_plane):
-            hid_codes = work.tile([P, ROUND, F_PASSES, P], U32, align_bytes=64, tag="hid_codes")
-            hid_plane = work.tile([P, ROUND, F_PASSES, P], U8, align_bytes=64, tag="hid_plane")
-            for pair in range(ROUND // 2):
-                hid_grouped = work.tile([P, 2, F_PASSES, P * 4], BF16, align_bytes=64, tag="hid_grouped")
-                for jj in range(2):
-                    j = pair * 2 + jj
-                    toks = slice(j * P, (j + 1) * P)
-                    hid_sorted = work.tile([P, F_PASSES, K_PASS], BF16, tag="hid_sorted", bufs=4)
-                    for g in range(F_PASSES):
-                        cols = slice(g * K_PASS, (g + 1) * K_PASS)
-                        acc1 = psum.tile([P, 512], F32, tag="acc1", bufs=3)
-                        nc.tensor.matmul_mx(
-                            out=acc1[:],
-                            lhsT=hq_codes[:, toks].bitcast(FP8X4),
-                            lhsT_scale=hq_plane[:, toks],
-                            rhs=w1_codes[:, cols].bitcast(FP8X4),
-                            rhs_scale=w1_plane[:, cols],
-                            start=True,
-                            stop=True,
-                        )
-                        nc.vector.tensor_tensor(
-                            out=hid_sorted[:, g, :].rearrange("k (u p e) -> k u p e", u=2, e=2),
-                            in0=acc1[:].rearrange("k (p u e) -> k u p e", u=2, e=2),
-                            in1=b1_sorted[:, cols].rearrange("k (u p e) -> k u p e", u=2, e=2),
-                            op=ALU.add,
-                        )
-                    hidT = psum.tile([P, F_PASSES, 2, P], F32, tag="hidT", bufs=2)
-                    for g in range(F_PASSES):
-                        words = hid_sorted[:, g, :].bitcast(F32)
-                        for u in range(2):
-                            nc.tensor.transpose(hidT[:, g, u, :], words[:, u * P : (u + 1) * P], ident[:])
-                    for g in range(F_PASSES):
-                        nc.scalar.activation(
-                            out=hid_grouped[:, jj, g, :].rearrange("p (k u e) -> p k u e", u=2, e=2),
-                            in_=hidT[:, g, :, :].bitcast(BF16).rearrange("p u (k e) -> p k u e", e=2),
-                            func=FUNC.Relu,
-                        )
-                nc.vector.quantize_mx(
-                    out=hid_codes[:, pair * 2 : pair * 2 + 2, :, :]
-                    .rearrange("p j g k -> p (j g k)")
-                    .bitcast(FP8X4),
-                    scales=hid_plane[:, pair * 2 : pair * 2 + 2, :, :].rearrange("p j g k -> p (j g k)"),
-                    in_=hid_grouped[:].rearrange("p j g c -> p (j g c)"),
+        def quantise_h(r):
+            codes = work.tile([P, ROUND_TOKENS], U32, align_bytes=64, tag="hq_codes")
+            plane = work.tile([P, ROUND_TOKENS], U8, align_bytes=64, tag="hq_plane")
+            nc.vector.quantize_mx(out=codes[:].bitcast(FP8X4), scales=plane[:], in_=h_grouped[r][:])
+            hq[r] = (codes, plane)
+
+        def first_matmul(r):
+            codes, plane = hq[r]
+            by_unit = work.tile([P, F_CHUNKS, ROUND_TOKENS], BF16, tag="hid_by_unit")
+            hid_by_unit[r] = by_unit
+            for j in range(F_CHUNKS):
+                units = slice(j * P, (j + 1) * P)
+                acc1 = psum.tile([P, ROUND_TOKENS], F32, tag="bank")
+                nc.tensor.matmul_mx(
+                    out=acc1[:],
+                    lhsT=w1_codes[:, units].bitcast(FP8X4),
+                    lhsT_scale=w1_plane[:, units],
+                    rhs=codes[:].bitcast(FP8X4),
+                    rhs_scale=plane[:],
+                    start=True,
+                    stop=True,
                 )
-            return hid_codes, hid_plane
+                if j % 2 == 0:
+                    nc.scalar.activation(
+                        out=by_unit[:, j, :], in_=acc1[:], func=FUNC.Relu, bias=b1_col[:, j : j + 1], scale=1.0
+                    )
+                else:
+                    nc.vector.tensor_scalar(
+                        out=by_unit[:, j, :], in0=acc1[:], scalar1=b1_col[:, j : j + 1], scalar2=0.0,
+                        op0=ALU.add, op1=ALU.max,
+                    )
 
-        def residual_plus_b2(r):
-            hb = work.tile([P, ROUND, D], F32, tag="hb", bufs=3)
-            for j in range(ROUND):
-                nc.gpsimd.tensor_tensor(out=hb[:, j, :], in0=h_sb[:, r * ROUND + j, :], in1=b2_all, op=ALU.add)
-            return hb
+        def hidden_to_tokens(r):
+            hid_sorted[r] = []
+            for k in range(ROUND):
+                by_token = psum.tile([P, F], BF16, tag="bank")
+                for j in range(F_CHUNKS):
+                    nc.tensor.transpose(
+                        by_token[:, j * P : (j + 1) * P], hid_by_unit[r][:, j, k * P : (k + 1) * P], ident_bf[:]
+                    )
+                in_order = work.tile([P, F], BF16, tag="hid_sorted", bufs=ROUND)
+                nc.scalar.copy(
+                    out=in_order[:].bitcast(F32).rearrange("k (g u p) -> k g u p", g=F_PASSES, u=2),
+                    in_=by_token[:].bitcast(F32).rearrange("k (g p u) -> k g u p", g=F_PASSES, u=2),
+                )
+                hid_sorted[r].append(in_order)
 
-        def output(r, hid_codes, hid_plane, hb):
-            resid = work.tile([P, ROUND, D], F32, tag="resid")
-            sums = work.tile([P, ROUND], F32, tag="sums")
-            neg_mean = work.tile([P, ROUND], F32, tag="neg_mean")
-            sq_sums = work.tile([P, ROUND], F32, tag="sq_sums")
-            std = work.tile([P, ROUND], F32, tag="std")
-            rstd = work.tile([P, ROUND], F32, tag="rstd")
-            for j in range(ROUND):
-                acc2 = psum.tile([P, D], F32, tag="acc2", bufs=2)
+        def hidden_to_words(r):
+            hid_grouped[r] = []
+            for pair in range(ROUND // 2):
+                grouped = work.tile([P, 2, F_PASSES, P * 4], BF16, align_bytes=64, tag="hid_grouped")
+                hid_grouped[r].append(grouped)
+                for kk in range(2):
+                    words = hid_sorted[r][pair * 2 + kk][:].bitcast(F32)
+                    hidT = psum.tile([P, F_PASSES, 2, P], F32, tag="bank")
+                    for g in range(F_PASSES):
+                        for u in range(2):
+                            first = (g * 2 + u) * P
+                            nc.tensor.transpose(hidT[:, g, u, :], words[:, first : first + P], ident[:])
+                    nc.scalar.copy(
+                        out=grouped[:, kk, :, :].bitcast(F32).rearrange("p g (k u) -> p g k u", u=2),
+                        in_=hidT[:].rearrange("p g u k -> p g k u"),
+                    )
+
+        def quantise_hidden(r):
+            codes = work.tile([P, ROUND, F_PASSES, P], U32, align_bytes=64, tag="hid_codes")
+            plane = work.tile([P, ROUND, F_PASSES, P], U8, align_bytes=64, tag="hid_plane")
+            hidq[r] = (codes, plane)
+            for pair in range(ROUND // 2):
+                tiles = slice(pair * 2, pair * 2 + 2)
+                nc.vector.quantize_mx(
+                    out=codes[:, tiles, :, :].rearrange("p j g k -> p (j g k)").bitcast(FP8X4),
+                    scales=plane[:, tiles, :, :].rearrange("p j g k -> p (j g k)"),
+                    in_=hid_grouped[r][pair][:].rearrange("p j g c -> p (j g c)"),
+                )
+
+        def second_matmul(r):
+            codes, plane = hidq[r]
+            sums = work.tile([P, ROUND], F32, tag="sums", bufs=3)
+            neg_mean = work.tile([P, ROUND], F32, tag="neg_mean", bufs=3)
+            sq_sums = work.tile([P, ROUND], F32, tag="sq_sums", bufs=3)
+            stats[r] = (neg_mean, sq_sums)
+            resid[r] = []
+            for k in range(ROUND):
+                acc2 = psum.tile([P, D], F32, tag="bank")
                 for g in range(F_PASSES):
                     nc.tensor.matmul_mx(
                         out=acc2[:],
-                        lhsT=hid_codes[:, j, g, :].bitcast(FP8X4),
-                        lhsT_scale=hid_plane[:, j, g, :],
+                        lhsT=codes[:, k, g, :].bitcast(FP8X4),
+                        lhsT_scale=plane[:, k, g, :],
                         rhs=w2_codes[:, g, :].bitcast(FP8X4),
                         rhs_scale=w2_plane[:, g, :],
                         start=(g == 0),
                         stop=(g == F_PASSES - 1),
                     )
+                res = work.tile([P, D], F32, tag="resid", bufs=ROUND)
+                resid[r].append(res)
                 nc.vector.scalar_tensor_tensor(
-                    out=resid[:, j, :], in0=acc2[:], scalar=1.0, in1=hb[:, j, :],
-                    op0=ALU.mult, op1=ALU.add, accum_out=sums[:, j : j + 1],
+                    out=res[:], in0=acc2[:], scalar=1.0, in1=hb_sb[:, r * ROUND + k, :],
+                    op0=ALU.mult, op1=ALU.add, accum_out=sums[:, k : k + 1],
                 )
-            nc.vector.tensor_scalar_mul(out=neg_mean[:], in0=sums[:], scalar1=-1.0 / D)
-            for j in range(ROUND):
+                nc.vector.tensor_scalar_mul(out=neg_mean[:, k : k + 1], in0=sums[:, k : k + 1], scalar1=-1.0 / D)
                 squares = work.tile([P, D], BF16, tag="squares")
                 nc.scalar.activation(
-                    out=squares[:], in_=resid[:, j, :], func=FUNC.Square,
-                    bias=neg_mean[:, j : j + 1], scale=1.0, accum_out=sq_sums[:, j : j + 1],
+                    out=squares[:], in_=res[:], func=FUNC.Square,
+                    bias=neg_mean[:, k : k + 1], scale=1.0, accum_out=sq_sums[:, k : k + 1],
                 )
+
+        def centre_and_gain(r):
+            neg_mean, sq_sums = stats[r]
+            std = work.tile([P, ROUND], F32, tag="std", bufs=3)
             nc.scalar.activation(out=std[:], in_=sq_sums[:], func=FUNC.Sqrt, bias=EPS, scale=1.0 / D)
-            nc.vector.reciprocal(out=rstd[:], in_=std[:])
-            for j in range(ROUND):
-                scaled = work.tile([P, D], F32, tag="scaled", bufs=3)
+            scaled[r] = [std]
+            for k in range(ROUND):
+                gained = work.tile([P, D], F32, tag="scaled", bufs=ROUND)
+                scaled[r].append(gained)
                 nc.vector.scalar_tensor_tensor(
-                    out=scaled[:], in0=resid[:, j, :], scalar=neg_mean[:, j : j + 1], in1=g2_all,
+                    out=gained[:], in0=resid[r][k][:], scalar=neg_mean[:, k : k + 1], in1=g2_all,
                     op0=ALU.add, op1=ALU.mult,
                 )
-                normed = work.tile([P, D], F32, tag="normed", bufs=4)
+
+        def finish(r):
+            rstd = work.tile([P, ROUND], F32, tag="rstd", bufs=3)
+            nc.vector.reciprocal(out=rstd[:], in_=scaled[r][0][:])
+            for k in range(ROUND):
+                normed = work.tile([P, D], F32, tag="normed", bufs=ROUND)
                 nc.vector.scalar_tensor_tensor(
-                    out=normed[:], in0=scaled[:], scalar=rstd[:, j : j + 1], in1=beta2_all,
+                    out=normed[:], in0=scaled[r][1 + k][:], scalar=rstd[:, k : k + 1], in1=beta2_all,
                     op0=ALU.mult, op1=ALU.add,
                 )
-                nc.sync.dma_start(out=out_rows[:, r * ROUND + j, :], in_=normed[:])
+                nc.sync.dma_start(out=out_rows[:, r * ROUND + k, :], in_=normed[:])
 
-        quantised_h = quantise_h(0)
-        for r in range(ROUNDS):
-            this_h = quantised_h
-            if r + 1 < ROUNDS:
-                quantised_h = quantise_h(r + 1)
-            hb = residual_plus_b2(r)
-            hid_codes, hid_plane = hidden(this_h[0], this_h[1])
-            output(r, hid_codes, hid_plane, hb)
+        def live(r):
+            return 0 <= r < ROUNDS
+
+        transpose_h(0)
+        quantise_h(0)
+        prepare_vectors()
+        for step in range(-1, ROUNDS + 2):
+            if live(step + 1):
+                first_matmul(step + 1)
+            if live(step - 1):
+                quantise_hidden(step - 1)
+            if live(step - 2):
+                finish(step - 2)
+            if live(step + 2):
+                transpose_h(step + 2)
+            if live(step):
+                hidden_to_tokens(step)
+            if live(step + 2):
+                quantise_h(step + 2)
+            if live(step - 1):
+                second_matmul(step - 1)
+            if live(step):
+                hidden_to_words(step)
+            if live(step - 1):
+                centre_and_gain(step - 1)

@@ -18,11 +18,11 @@ D = 512
 F = 1024
 K_PASS = 512
 F_PASSES = F // K_PASS
-F_CHUNKS = F // P
 TILES = TOKENS // P
 ROUND = 4
 ROUND_TOKENS = ROUND * P
 ROUNDS = TILES // ROUND
+HB_ON_VECTOR = 2
 EPS = 1e-3
 
 FLOPS = 2 * TOKENS * D * F * 2
@@ -41,13 +41,14 @@ def tile_ffnn_encoder_pc_t_kernel(
         psum = ctx.enter_context(tc.psum_pool(name="psum", bufs=8))
 
         h_sb = const.tile([P, TILES, D], BF16)
-        hb_sb = const.tile([P, TILES, D], F32)
-        w1_codes = const.tile([P, F], U32, align_bytes=64)
-        w1_plane = const.tile([P, F], U8, align_bytes=64)
+        w1_codes_raw = const.tile([P, F], U32, align_bytes=64)
+        w1_plane_raw = const.tile([P, F], U8, align_bytes=64)
+        w1_codes = const.tile([P, F_PASSES, 4, P], U32, align_bytes=64)
+        w1_plane = const.tile([P, F_PASSES, 4, P], U8, align_bytes=64)
         w2_codes = const.tile([P, F_PASSES, D], U32, align_bytes=64)
         w2_plane = const.tile([P, F_PASSES, D], U8, align_bytes=64)
-        b1_rows = const.tile([P, P], BF16)
-        b1_col = const.tile([P, F_CHUNKS], F32)
+        b1_bf = const.tile([P, F_PASSES, 4], BF16)
+        b1_col = const.tile([P, F_PASSES, 4], F32)
         vec_rows = const.tile([P, 3 * D], BF16)
         spread = const.tile([P, 3 * D], F32)
         ones = const.tile([P, P], BF16)
@@ -56,9 +57,8 @@ def tile_ffnn_encoder_pc_t_kernel(
         one_col = const.tile([P, 1], F32)
         sqrt_warm = const.tile([P, 1], F32)
 
-        nc.vector.memset(b1_rows[:].bitcast(I32), 0)
         nc.vector.memset(vec_rows[:].bitcast(I32), 0)
-        nc.vector.memset(w1_plane[:].bitcast(I32), 0)
+        nc.vector.memset(w1_plane_raw[:].bitcast(I32), 0)
         nc.vector.memset(w2_plane[:].bitcast(I32), 0)
         nc.vector.memset(ones[:], 1.0)
         nc.vector.memset(one_col[:], 1.0)
@@ -71,18 +71,18 @@ def tile_ffnn_encoder_pc_t_kernel(
             nc.sync.dma_start(out=h_sb[:, tiles, :], in_=h_rows[:, tiles, :])
 
         load_h(0)
-        nc.sync.dma_start(out=b1_rows[0:F_CHUNKS, :], in_=b1.rearrange("(j m) -> j m", m=P))
+        nc.sync.dma_start(out=b1_bf[:], in_=b1.rearrange("(g p t) -> p g t", p=P, t=4))
         for i, vec in enumerate((b2, g2, beta2)):
             nc.sync.dma_start(
                 out=vec_rows[0:1, i * D : (i + 1) * D], in_=vec.rearrange("(o n) -> o n", o=1)
             )
         for row in range(4):
             nc.sync.dma_start(
-                out=w1_plane[row:P:32, :].bitcast(I32),
+                out=w1_plane_raw[row:P:32, :].bitcast(I32),
                 in_=W1_scales[0, row:16:4, :].bitcast(I32),
             )
         nc.sync.dma_start(
-            out=w1_codes[:].bitcast(I32),
+            out=w1_codes_raw[:].bitcast(I32),
             in_=W1_words[0].rearrange("p n t -> p (n t)").bitcast(I32),
         )
         load_h(1)
@@ -105,23 +105,29 @@ def tile_ffnn_encoder_pc_t_kernel(
         beta2_all = spread[:, 2 * D : 3 * D]
 
         def prepare_vectors():
-            flipped = psum.tile([P, F], BF16, tag="bank")
-            nc.tensor.transpose(flipped[:, 0:P], b1_rows[:], ident_bf[:])
-            nc.vector.tensor_copy(out=b1_col[:], in_=flipped[:, 0:F_CHUNKS])
+            nc.vector.tensor_copy(out=b1_col[:], in_=b1_bf[:])
+            for g in range(F_PASSES):
+                units = slice(g * K_PASS, (g + 1) * K_PASS)
+                nc.vector.tensor_copy(
+                    out=w1_codes[:, g, :, :].bitcast(I32),
+                    in_=w1_codes_raw[:, units].bitcast(I32).rearrange("p (m t) -> p t m", t=4),
+                )
+                nc.vector.tensor_copy(
+                    out=w1_plane[:, g, :, :],
+                    in_=w1_plane_raw[:, units].rearrange("p (m t) -> p t m", t=4),
+                )
             for i in range(3):
                 cols = slice(i * D, (i + 1) * D)
                 bank = psum.tile([P, D], F32, tag="bank")
                 nc.tensor.matmul(out=bank[:], lhsT=ones[:], rhs=vec_rows[:, cols], start=True, stop=True)
                 nc.vector.tensor_copy(out=spread[:, cols], in_=bank[:])
-            for n in range(TILES):
-                nc.gpsimd.tensor_tensor(out=hb_sb[:, n, :], in0=h_sb[:, n, :], in1=b2_all, op=ALU.add)
 
         h_grouped = {}
         hq = {}
         hid_by_unit = {}
-        hid_sorted = {}
         hid_grouped = {}
         hidq = {}
+        hb = {}
         resid = {}
         stats = {}
         scaled = {}
@@ -150,76 +156,62 @@ def tile_ffnn_encoder_pc_t_kernel(
 
         def first_matmul(r):
             codes, plane = hq[r]
-            by_unit = work.tile([P, F_CHUNKS, ROUND_TOKENS], BF16, tag="hid_by_unit")
-            hid_by_unit[r] = by_unit
-            for j in range(F_CHUNKS):
-                units = slice(j * P, (j + 1) * P)
-                acc1 = psum.tile([P, ROUND_TOKENS], F32, tag="bank")
-                nc.tensor.matmul_mx(
-                    out=acc1[:],
-                    lhsT=w1_codes[:, units].bitcast(FP8X4),
-                    lhsT_scale=w1_plane[:, units],
-                    rhs=codes[:].bitcast(FP8X4),
-                    rhs_scale=plane[:],
-                    start=True,
-                    stop=True,
-                )
-                if j % 2 == 0:
+            hid_by_unit[r] = []
+            for g in range(F_PASSES):
+                by_unit = work.tile([P, 4, ROUND_TOKENS], BF16, tag="hid_by_unit", bufs=4)
+                hid_by_unit[r].append(by_unit)
+                for t in range(4):
+                    acc1 = psum.tile([P, ROUND_TOKENS], F32, tag="bank")
+                    nc.tensor.matmul_mx(
+                        out=acc1[:],
+                        lhsT=w1_codes[:, g, t, :].bitcast(FP8X4),
+                        lhsT_scale=w1_plane[:, g, t, :],
+                        rhs=codes[:].bitcast(FP8X4),
+                        rhs_scale=plane[:],
+                        start=True,
+                        stop=True,
+                    )
                     nc.scalar.activation(
-                        out=by_unit[:, j, :], in_=acc1[:], func=FUNC.Relu, bias=b1_col[:, j : j + 1], scale=1.0
+                        out=by_unit[:, t, :], in_=acc1[:], func=FUNC.Relu, bias=b1_col[:, g, t : t + 1], scale=1.0
                     )
-                else:
-                    nc.vector.tensor_scalar(
-                        out=by_unit[:, j, :], in0=acc1[:], scalar1=b1_col[:, j : j + 1], scalar2=0.0,
-                        op0=ALU.add, op1=ALU.max,
-                    )
-
-        def hidden_to_tokens(r):
-            hid_sorted[r] = []
-            for k in range(ROUND):
-                by_token = psum.tile([P, F], BF16, tag="bank")
-                for j in range(F_CHUNKS):
-                    nc.tensor.transpose(
-                        by_token[:, j * P : (j + 1) * P], hid_by_unit[r][:, j, k * P : (k + 1) * P], ident_bf[:]
-                    )
-                in_order = work.tile([P, F], BF16, tag="hid_sorted", bufs=ROUND)
-                nc.scalar.copy(
-                    out=in_order[:].bitcast(F32).rearrange("k (g u p) -> k g u p", g=F_PASSES, u=2),
-                    in_=by_token[:].bitcast(F32).rearrange("k (g p u) -> k g u p", g=F_PASSES, u=2),
-                )
-                hid_sorted[r].append(in_order)
 
         def hidden_to_words(r):
             hid_grouped[r] = []
-            for pair in range(ROUND // 2):
-                grouped = work.tile([P, 2, F_PASSES, P * 4], BF16, align_bytes=64, tag="hid_grouped")
+            for g in range(F_PASSES):
+                grouped = work.tile([P, ROUND_TOKENS, 4], BF16, align_bytes=64, tag="hid_grouped", bufs=3)
                 hid_grouped[r].append(grouped)
-                for kk in range(2):
-                    words = hid_sorted[r][pair * 2 + kk][:].bitcast(F32)
-                    hidT = psum.tile([P, F_PASSES, 2, P], F32, tag="bank")
-                    for g in range(F_PASSES):
-                        for u in range(2):
-                            first = (g * 2 + u) * P
-                            nc.tensor.transpose(hidT[:, g, u, :], words[:, first : first + P], ident[:])
-                    nc.scalar.copy(
-                        out=grouped[:, kk, :, :].bitcast(F32).rearrange("p g (k u) -> p g k u", u=2),
-                        in_=hidT[:].rearrange("p g u k -> p g k u"),
-                    )
-
-        def quantise_hidden(r):
-            codes = work.tile([P, ROUND, F_PASSES, P], U32, align_bytes=64, tag="hid_codes")
-            plane = work.tile([P, ROUND, F_PASSES, P], U8, align_bytes=64, tag="hid_plane")
-            hidq[r] = (codes, plane)
-            for pair in range(ROUND // 2):
-                tiles = slice(pair * 2, pair * 2 + 2)
-                nc.vector.quantize_mx(
-                    out=codes[:, tiles, :, :].rearrange("p j g k -> p (j g k)").bitcast(FP8X4),
-                    scales=plane[:, tiles, :, :].rearrange("p j g k -> p (j g k)"),
-                    in_=hid_grouped[r][pair][:].rearrange("p j g c -> p (j g c)"),
+                nc.vector.tensor_copy(
+                    out=grouped[:].rearrange("p (c i) t -> p c t i", i=4),
+                    in_=hid_by_unit[r][g][:].rearrange("p t (c i) -> p c t i", i=4),
                 )
 
+        def quantise_hidden(r):
+            hidq[r] = []
+            for g in range(F_PASSES):
+                codes = work.tile([P, ROUND_TOKENS], U32, align_bytes=64, tag="hid_codes", bufs=4)
+                plane = work.tile([P, ROUND_TOKENS], U8, align_bytes=64, tag="hid_plane", bufs=4)
+                hidq[r].append((codes, plane))
+                nc.vector.quantize_mx(
+                    out=codes[:].bitcast(FP8X4),
+                    scales=plane[:],
+                    in_=hid_grouped[r][g][:].rearrange("p k t -> p (k t)"),
+                )
+
+        def residual_and_bias(r):
+            hb[r] = []
+            for k in range(ROUND):
+                h_tile = h_sb[:, r * ROUND + k, :]
+                both = work.tile([P, D], F32, tag="hb", bufs=3 * ROUND)
+                hb[r].append(both)
+                if r < HB_ON_VECTOR:
+                    nc.vector.tensor_tensor(out=both[:], in0=h_tile, in1=b2_all, op=ALU.add)
+                else:
+                    bank = psum.tile([P, D], F32, tag="bank")
+                    nc.tensor.matmul(out=bank[:], lhsT=ident_bf[:], rhs=h_tile, start=True, stop=False)
+                    nc.tensor.matmul(out=bank[:], lhsT=ones[:], rhs=vec_rows[:, 0:D], start=False, stop=True)
+                    nc.scalar.copy(out=both[:], in_=bank[:])
+
         def second_matmul(r):
-            codes, plane = hidq[r]
             sums = work.tile([P, ROUND], F32, tag="sums", bufs=3)
             neg_mean = work.tile([P, ROUND], F32, tag="neg_mean", bufs=3)
             sq_sums = work.tile([P, ROUND], F32, tag="sq_sums", bufs=3)
@@ -230,17 +222,17 @@ def tile_ffnn_encoder_pc_t_kernel(
                 for g in range(F_PASSES):
                     nc.tensor.matmul_mx(
                         out=acc2[:],
-                        lhsT=codes[:, k, g, :].bitcast(FP8X4),
-                        lhsT_scale=plane[:, k, g, :],
+                        lhsT=hidq[r][g][0][:, k * P : (k + 1) * P].bitcast(FP8X4),
+                        lhsT_scale=hidq[r][g][1][:, k * P : (k + 1) * P],
                         rhs=w2_codes[:, g, :].bitcast(FP8X4),
                         rhs_scale=w2_plane[:, g, :],
                         start=(g == 0),
                         stop=(g == F_PASSES - 1),
                     )
-                res = work.tile([P, D], F32, tag="resid", bufs=ROUND)
+                res = work.tile([P, D], F32, tag="resid", bufs=2 * ROUND)
                 resid[r].append(res)
                 nc.vector.scalar_tensor_tensor(
-                    out=res[:], in0=acc2[:], scalar=1.0, in1=hb_sb[:, r * ROUND + k, :],
+                    out=res[:], in0=acc2[:], scalar=1.0, in1=hb[r][k][:],
                     op0=ALU.mult, op1=ALU.add, accum_out=sums[:, k : k + 1],
                 )
                 nc.vector.tensor_scalar_mul(out=neg_mean[:, k : k + 1], in0=sums[:, k : k + 1], scalar1=-1.0 / D)
@@ -256,7 +248,7 @@ def tile_ffnn_encoder_pc_t_kernel(
             nc.scalar.activation(out=std[:], in_=sq_sums[:], func=FUNC.Sqrt, bias=EPS, scale=1.0 / D)
             scaled[r] = [std]
             for k in range(ROUND):
-                gained = work.tile([P, D], F32, tag="scaled", bufs=ROUND)
+                gained = work.tile([P, D], F32, tag="scaled", bufs=2 * ROUND)
                 scaled[r].append(gained)
                 nc.vector.scalar_tensor_tensor(
                     out=gained[:], in0=resid[r][k][:], scalar=neg_mean[:, k : k + 1], in1=g2_all,
@@ -267,7 +259,7 @@ def tile_ffnn_encoder_pc_t_kernel(
             rstd = work.tile([P, ROUND], F32, tag="rstd", bufs=3)
             nc.vector.reciprocal(out=rstd[:], in_=scaled[r][0][:])
             for k in range(ROUND):
-                normed = work.tile([P, D], F32, tag="normed", bufs=ROUND)
+                normed = work.tile([P, D], F32, tag="normed", bufs=ROUND + 2)
                 nc.vector.scalar_tensor_tensor(
                     out=normed[:], in0=scaled[r][1 + k][:], scalar=rstd[:, k : k + 1], in1=beta2_all,
                     op0=ALU.mult, op1=ALU.add,
@@ -280,22 +272,23 @@ def tile_ffnn_encoder_pc_t_kernel(
         transpose_h(0)
         quantise_h(0)
         prepare_vectors()
-        for step in range(-1, ROUNDS + 2):
+        residual_and_bias(0)
+        for step in range(-1, ROUNDS + 1):
             if live(step + 1):
                 first_matmul(step + 1)
-            if live(step - 1):
-                quantise_hidden(step - 1)
-            if live(step - 2):
-                finish(step - 2)
             if live(step + 2):
                 transpose_h(step + 2)
             if live(step):
-                hidden_to_tokens(step)
+                second_matmul(step)
+            if live(step + 2):
+                residual_and_bias(step + 2)
+            if live(step + 1):
+                hidden_to_words(step + 1)
             if live(step + 2):
                 quantise_h(step + 2)
-            if live(step - 1):
-                second_matmul(step - 1)
             if live(step):
-                hidden_to_words(step)
+                centre_and_gain(step)
+            if live(step + 1):
+                quantise_hidden(step + 1)
             if live(step - 1):
-                centre_and_gain(step - 1)
+                finish(step - 1)

@@ -22,7 +22,6 @@ TILES = TOKENS // P
 ROUND = 4
 ROUND_TOKENS = ROUND * P
 ROUNDS = TILES // ROUND
-HB_ON_VECTOR = 2
 EPS = 1e-3
 
 FLOPS = 2 * TOKENS * D * F * 2
@@ -38,7 +37,8 @@ def tile_ffnn_encoder_pc_t_kernel(
     with ExitStack() as ctx:
         const = ctx.enter_context(tc.tile_pool(name="const", bufs=1))
         work = ctx.enter_context(tc.tile_pool(name="work", bufs=2))
-        psum = ctx.enter_context(tc.psum_pool(name="psum", bufs=8))
+        psum = ctx.enter_context(tc.psum_pool(name="psum", bufs=6))
+        psum_const = ctx.enter_context(tc.psum_pool(name="psum_const", bufs=1))
 
         h_sb = const.tile([P, TILES, D], BF16)
         w1_codes_raw = const.tile([P, F], U32, align_bytes=64)
@@ -50,15 +50,17 @@ def tile_ffnn_encoder_pc_t_kernel(
         b1_bf = const.tile([P, F_PASSES, 4], BF16)
         b1_col = const.tile([P, F_PASSES, 4], F32)
         vec_rows = const.tile([P, 3 * D], BF16)
-        spread = const.tile([P, 3 * D], F32)
+        b2_all = const.tile([P, D], F32)
+        g2_all = psum_const.tile([P, D], F32, tag="g2_all")
+        beta2_all = psum_const.tile([P, D], F32, tag="beta2_all")
         ones = const.tile([P, P], BF16)
         ident = const.tile([P, P], F32)
         ident_bf = const.tile([P, P], BF16)
         one_col = const.tile([P, 1], F32)
         sqrt_warm = const.tile([P, 1], F32)
 
-        nc.vector.memset(vec_rows[:].bitcast(I32), 0)
         nc.vector.memset(w1_plane_raw[:].bitcast(I32), 0)
+        nc.vector.memset(vec_rows[:].bitcast(I32), 0)
         nc.vector.memset(w2_plane[:].bitcast(I32), 0)
         nc.vector.memset(ones[:], 1.0)
         nc.vector.memset(one_col[:], 1.0)
@@ -71,11 +73,6 @@ def tile_ffnn_encoder_pc_t_kernel(
             nc.sync.dma_start(out=h_sb[:, tiles, :], in_=h_rows[:, tiles, :])
 
         load_h(0)
-        nc.sync.dma_start(out=b1_bf[:], in_=b1.rearrange("(g p t) -> p g t", p=P, t=4))
-        for i, vec in enumerate((b2, g2, beta2)):
-            nc.sync.dma_start(
-                out=vec_rows[0:1, i * D : (i + 1) * D], in_=vec.rearrange("(o n) -> o n", o=1)
-            )
         for row in range(4):
             nc.sync.dma_start(
                 out=w1_plane_raw[row:P:32, :].bitcast(I32),
@@ -85,6 +82,11 @@ def tile_ffnn_encoder_pc_t_kernel(
             out=w1_codes_raw[:].bitcast(I32),
             in_=W1_words[0].rearrange("p n t -> p (n t)").bitcast(I32),
         )
+        nc.sync.dma_start(out=b1_bf[:], in_=b1.rearrange("(g p t) -> p g t", p=P, t=4))
+        for i, vec in enumerate((b2, g2, beta2)):
+            nc.sync.dma_start(
+                out=vec_rows[0:1, i * D : (i + 1) * D], in_=vec.rearrange("(o n) -> o n", o=1)
+            )
         load_h(1)
         for g in range(F_PASSES):
             for row in range(4):
@@ -100,195 +102,274 @@ def tile_ffnn_encoder_pc_t_kernel(
         for r in range(2, ROUNDS):
             load_h(r)
 
-        b2_all = spread[:, 0:D]
-        g2_all = spread[:, D : 2 * D]
-        beta2_all = spread[:, 2 * D : 3 * D]
-
-        def prepare_vectors():
-            nc.vector.tensor_copy(out=b1_col[:], in_=b1_bf[:])
+        def reorder_w1():
             for g in range(F_PASSES):
                 units = slice(g * K_PASS, (g + 1) * K_PASS)
-                nc.vector.tensor_copy(
-                    out=w1_codes[:, g, :, :].bitcast(I32),
-                    in_=w1_codes_raw[:, units].bitcast(I32).rearrange("p (m t) -> p t m", t=4),
-                )
                 nc.vector.tensor_copy(
                     out=w1_plane[:, g, :, :],
                     in_=w1_plane_raw[:, units].rearrange("p (m t) -> p t m", t=4),
                 )
-            for i in range(3):
+                nc.vector.tensor_copy(
+                    out=w1_codes[:, g, :, :].bitcast(I32),
+                    in_=w1_codes_raw[:, units].bitcast(I32).rearrange("p (m t) -> p t m", t=4),
+                )
+            nc.vector.tensor_copy(out=b1_col[:], in_=b1_bf[:])
+
+        def spread_vectors():
+            bank = psum.tile([P, D], F32, tag="bank")
+            for i, spread in enumerate((bank, g2_all, beta2_all)):
                 cols = slice(i * D, (i + 1) * D)
-                bank = psum.tile([P, D], F32, tag="bank")
-                nc.tensor.matmul(out=bank[:], lhsT=ones[:], rhs=vec_rows[:, cols], start=True, stop=True)
-                nc.vector.tensor_copy(out=spread[:, cols], in_=bank[:])
+                nc.tensor.matmul(out=spread[:], lhsT=ones[:], rhs=vec_rows[:, cols], start=True, stop=True)
+            nc.vector.tensor_copy(out=b2_all[:], in_=bank[:])
 
         h_grouped = {}
         hq = {}
+        products = {}
         hid_by_unit = {}
         hid_grouped = {}
         hidq = {}
         hb = {}
         resid = {}
-        stats = {}
+        sums = {}
+        neg_mean = {}
+        sq_sums = {}
+        std = {}
+        rstd = {}
         scaled = {}
 
-        def transpose_h(r):
-            grouped = work.tile([P, ROUND_TOKENS * 4], BF16, align_bytes=64, tag="h_grouped")
-            h_grouped[r] = grouped
-            for half in range(ROUND // 2):
-                hT = psum.tile([P, 2, 2, P], F32, tag="bank")
-                for j in range(2):
-                    words = h_sb[:, r * ROUND + half * 2 + j, :].bitcast(F32)
-                    for u in range(2):
-                        nc.tensor.transpose(hT[:, j, u, :], words[:, u : D // 2 : 2], ident[:])
-                nc.scalar.copy(
-                    out=grouped[:, half * 2 * P * 4 : (half + 1) * 2 * P * 4]
-                    .bitcast(F32)
-                    .rearrange("p (j k u) -> p j k u", j=2, u=2),
-                    in_=hT[:].rearrange("p j u k -> p j k u"),
-                )
+        def transpose_h(r, half):
+            if half == 0:
+                h_grouped[r] = work.tile([P, ROUND_TOKENS * 4], BF16, align_bytes=64, tag="h_grouped", bufs=3, name="h_grouped_tile")
+            hT = psum.tile([P, 2, 2, P], F32, tag="bank")
+            for j in range(2):
+                words = h_sb[:, r * ROUND + half * 2 + j, :].bitcast(F32)
+                for u in range(2):
+                    nc.tensor.transpose(hT[:, j, u, :], words[:, u : D // 2 : 2], ident[:])
+            nc.scalar.copy(
+                out=h_grouped[r][:, half * 2 * P * 4 : (half + 1) * 2 * P * 4]
+                .bitcast(F32)
+                .rearrange("p (j k u) -> p j k u", j=2, u=2),
+                in_=hT[:].rearrange("p j u k -> p j k u"),
+            )
 
         def quantise_h(r):
-            codes = work.tile([P, ROUND_TOKENS], U32, align_bytes=64, tag="hq_codes")
-            plane = work.tile([P, ROUND_TOKENS], U8, align_bytes=64, tag="hq_plane")
+            codes = work.tile([P, ROUND_TOKENS], U32, align_bytes=64, tag="hq_codes", bufs=3)
+            plane = work.tile([P, ROUND_TOKENS], U8, align_bytes=64, tag="hq_plane", bufs=3)
             nc.vector.quantize_mx(out=codes[:].bitcast(FP8X4), scales=plane[:], in_=h_grouped[r][:])
             hq[r] = (codes, plane)
 
-        def first_matmul(r):
+        def hidden_product(r, g, t):
             codes, plane = hq[r]
-            hid_by_unit[r] = []
-            for g in range(F_PASSES):
-                by_unit = work.tile([P, 4, ROUND_TOKENS], BF16, tag="hid_by_unit", bufs=4)
-                hid_by_unit[r].append(by_unit)
-                for t in range(4):
-                    acc1 = psum.tile([P, ROUND_TOKENS], F32, tag="bank")
-                    nc.tensor.matmul_mx(
-                        out=acc1[:],
-                        lhsT=w1_codes[:, g, t, :].bitcast(FP8X4),
-                        lhsT_scale=w1_plane[:, g, t, :],
-                        rhs=codes[:].bitcast(FP8X4),
-                        rhs_scale=plane[:],
-                        start=True,
-                        stop=True,
-                    )
-                    nc.scalar.activation(
-                        out=by_unit[:, t, :], in_=acc1[:], func=FUNC.Relu, bias=b1_col[:, g, t : t + 1], scale=1.0
-                    )
+            acc1 = psum.tile([P, ROUND_TOKENS], F32, tag="bank")
+            products[r, g, t] = acc1
+            nc.tensor.matmul_mx(
+                out=acc1[:],
+                lhsT=w1_codes[:, g, t, :].bitcast(FP8X4),
+                lhsT_scale=w1_plane[:, g, t, :],
+                rhs=codes[:].bitcast(FP8X4),
+                rhs_scale=plane[:],
+                start=True,
+                stop=True,
+            )
 
-        def hidden_to_words(r):
-            hid_grouped[r] = []
-            for g in range(F_PASSES):
-                grouped = work.tile([P, ROUND_TOKENS, 4], BF16, align_bytes=64, tag="hid_grouped", bufs=3)
-                hid_grouped[r].append(grouped)
+        def hidden_copy(r, g, t, engine):
+            if (r, g) not in hid_by_unit:
+                hid_by_unit[r, g] = work.tile([P, 4, ROUND_TOKENS], BF16, tag="hid_by_unit", bufs=6, name="by_unit_tile")
+            by_unit = hid_by_unit[r, g]
+            acc1 = products[r, g, t]
+            if engine == "vector":
+                nc.vector.tensor_scalar(
+                    out=by_unit[:, t, :], in0=acc1[:], scalar1=b1_col[:, g, t : t + 1], scalar2=0.0,
+                    op0=ALU.add, op1=ALU.max,
+                )
+            else:
+                nc.scalar.activation(
+                    out=by_unit[:, t, :], in_=acc1[:], func=FUNC.Relu, bias=b1_col[:, g, t : t + 1], scale=1.0
+                )
+
+        def hidden_to_words(r, g, engine):
+            grouped = work.tile([P, ROUND_TOKENS, 4], BF16, align_bytes=64, tag="hid_grouped", bufs=4)
+            hid_grouped[r, g] = grouped
+            if engine == "vector":
                 nc.vector.tensor_copy(
                     out=grouped[:].rearrange("p (c i) t -> p c t i", i=4),
-                    in_=hid_by_unit[r][g][:].rearrange("p t (c i) -> p c t i", i=4),
+                    in_=hid_by_unit[r, g][:].rearrange("p t (c i) -> p c t i", i=4),
                 )
-
-        def quantise_hidden(r):
-            hidq[r] = []
-            for g in range(F_PASSES):
-                codes = work.tile([P, ROUND_TOKENS], U32, align_bytes=64, tag="hid_codes", bufs=4)
-                plane = work.tile([P, ROUND_TOKENS], U8, align_bytes=64, tag="hid_plane", bufs=4)
-                hidq[r].append((codes, plane))
-                nc.vector.quantize_mx(
-                    out=codes[:].bitcast(FP8X4),
-                    scales=plane[:],
-                    in_=hid_grouped[r][g][:].rearrange("p k t -> p (k t)"),
-                )
-
-        def residual_and_bias(r):
-            hb[r] = []
-            for k in range(ROUND):
-                h_tile = h_sb[:, r * ROUND + k, :]
-                both = work.tile([P, D], F32, tag="hb", bufs=3 * ROUND)
-                hb[r].append(both)
-                if r < HB_ON_VECTOR:
-                    nc.vector.tensor_tensor(out=both[:], in0=h_tile, in1=b2_all, op=ALU.add)
-                else:
-                    bank = psum.tile([P, D], F32, tag="bank")
-                    nc.tensor.matmul(out=bank[:], lhsT=ident_bf[:], rhs=h_tile, start=True, stop=False)
-                    nc.tensor.matmul(out=bank[:], lhsT=ones[:], rhs=vec_rows[:, 0:D], start=False, stop=True)
-                    nc.scalar.copy(out=both[:], in_=bank[:])
-
-        def second_matmul(r):
-            sums = work.tile([P, ROUND], F32, tag="sums", bufs=3)
-            neg_mean = work.tile([P, ROUND], F32, tag="neg_mean", bufs=3)
-            sq_sums = work.tile([P, ROUND], F32, tag="sq_sums", bufs=3)
-            stats[r] = (neg_mean, sq_sums)
-            resid[r] = []
-            for k in range(ROUND):
-                acc2 = psum.tile([P, D], F32, tag="bank")
-                for g in range(F_PASSES):
-                    nc.tensor.matmul_mx(
-                        out=acc2[:],
-                        lhsT=hidq[r][g][0][:, k * P : (k + 1) * P].bitcast(FP8X4),
-                        lhsT_scale=hidq[r][g][1][:, k * P : (k + 1) * P],
-                        rhs=w2_codes[:, g, :].bitcast(FP8X4),
-                        rhs_scale=w2_plane[:, g, :],
-                        start=(g == 0),
-                        stop=(g == F_PASSES - 1),
+            else:
+                for half in range(2):
+                    tokens = slice(half * ROUND_TOKENS // 2, (half + 1) * ROUND_TOKENS // 2)
+                    nc.gpsimd.tensor_scalar(
+                        out=grouped[:, tokens, :],
+                        in0=hid_by_unit[r, g][:, :, tokens].rearrange("p t k -> p k t"),
+                        scalar1=1.0, scalar2=0.0, op0=ALU.mult, op1=ALU.add,
                     )
-                res = work.tile([P, D], F32, tag="resid", bufs=2 * ROUND)
-                resid[r].append(res)
-                nc.vector.scalar_tensor_tensor(
-                    out=res[:], in0=acc2[:], scalar=1.0, in1=hb[r][k][:],
-                    op0=ALU.mult, op1=ALU.add, accum_out=sums[:, k : k + 1],
-                )
-                nc.vector.tensor_scalar_mul(out=neg_mean[:, k : k + 1], in0=sums[:, k : k + 1], scalar1=-1.0 / D)
-                squares = work.tile([P, D], BF16, tag="squares")
-                nc.scalar.activation(
-                    out=squares[:], in_=res[:], func=FUNC.Square,
-                    bias=neg_mean[:, k : k + 1], scale=1.0, accum_out=sq_sums[:, k : k + 1],
-                )
 
-        def centre_and_gain(r):
-            neg_mean, sq_sums = stats[r]
-            std = work.tile([P, ROUND], F32, tag="std", bufs=3)
-            nc.scalar.activation(out=std[:], in_=sq_sums[:], func=FUNC.Sqrt, bias=EPS, scale=1.0 / D)
-            scaled[r] = [std]
-            for k in range(ROUND):
-                gained = work.tile([P, D], F32, tag="scaled", bufs=2 * ROUND)
-                scaled[r].append(gained)
-                nc.vector.scalar_tensor_tensor(
-                    out=gained[:], in0=resid[r][k][:], scalar=neg_mean[:, k : k + 1], in1=g2_all,
-                    op0=ALU.add, op1=ALU.mult,
-                )
+        def quantise_hidden(r, g):
+            codes = work.tile([P, ROUND_TOKENS], U32, align_bytes=64, tag="hid_codes", bufs=6)
+            plane = work.tile([P, ROUND_TOKENS], U8, align_bytes=64, tag="hid_plane", bufs=6)
+            hidq[r, g] = (codes, plane)
+            nc.vector.quantize_mx(
+                out=codes[:].bitcast(FP8X4),
+                scales=plane[:],
+                in_=hid_grouped[r, g][:].rearrange("p k t -> p (k t)"),
+            )
 
-        def finish(r):
-            rstd = work.tile([P, ROUND], F32, tag="rstd", bufs=3)
-            nc.vector.reciprocal(out=rstd[:], in_=scaled[r][0][:])
-            for k in range(ROUND):
-                normed = work.tile([P, D], F32, tag="normed", bufs=ROUND + 2)
-                nc.vector.scalar_tensor_tensor(
-                    out=normed[:], in0=scaled[r][1 + k][:], scalar=rstd[:, k : k + 1], in1=beta2_all,
-                    op0=ALU.mult, op1=ALU.add,
+        def residual_and_bias(r, k, engine):
+            h_tile = h_sb[:, r * ROUND + k, :]
+            both = work.tile([P, D], F32, tag="hb", bufs=4 * ROUND)
+            hb[r, k] = both
+            if engine == "gpsimd":
+                nc.gpsimd.tensor_tensor(out=both[:], in0=h_tile, in1=b2_all[:], op=ALU.add)
+            elif engine == "vector":
+                nc.vector.tensor_tensor(out=both[:], in0=h_tile, in1=b2_all[:], op=ALU.add)
+            else:
+                bank = psum.tile([P, D], F32, tag="bank")
+                nc.tensor.matmul(out=bank[:], lhsT=ident_bf[:], rhs=h_tile, start=True, stop=False)
+                nc.tensor.matmul(out=bank[:], lhsT=ones[:], rhs=vec_rows[:, 0:D], start=False, stop=True)
+                nc.scalar.copy(out=both[:], in_=bank[:])
+
+        def add_up(r, k):
+            if k == 0:
+                sums[r] = work.tile([P, ROUND], F32, tag="sums", bufs=3, name="sums_tile")
+            acc2 = psum.tile([P, D], F32, tag="bank")
+            tokens = slice(k * P, (k + 1) * P)
+            for g in range(F_PASSES):
+                codes, plane = hidq[r, g]
+                nc.tensor.matmul_mx(
+                    out=acc2[:],
+                    lhsT=codes[:, tokens].bitcast(FP8X4),
+                    lhsT_scale=plane[:, tokens],
+                    rhs=w2_codes[:, g, :].bitcast(FP8X4),
+                    rhs_scale=w2_plane[:, g, :],
+                    start=(g == 0),
+                    stop=(g == F_PASSES - 1),
                 )
-                nc.sync.dma_start(out=out_rows[:, r * ROUND + k, :], in_=normed[:])
+            res = work.tile([P, D], F32, tag="resid", bufs=2 * ROUND)
+            resid[r, k] = res
+            nc.vector.scalar_tensor_tensor(
+                out=res[:], in0=acc2[:], scalar=1.0, in1=hb[r, k][:],
+                op0=ALU.mult, op1=ALU.add, accum_out=sums[r][:, k : k + 1],
+            )
+
+        def mean(r):
+            neg_mean[r] = work.tile([P, ROUND], F32, tag="neg_mean", bufs=3, name="neg_mean_tile")
+            nc.vector.tensor_scalar_mul(out=neg_mean[r][:], in0=sums[r][:], scalar1=-1.0 / D)
+
+        def square(r, k):
+            if k == 0:
+                sq_sums[r] = work.tile([P, ROUND], F32, tag="sq_sums", bufs=3, name="sq_sums_tile")
+            squares = work.tile([P, D], BF16, tag="squares")
+            nc.scalar.activation(
+                out=squares[:], in_=resid[r, k][:], func=FUNC.Square,
+                bias=sums[r][:, k : k + 1], scale=-float(D), accum_out=sq_sums[r][:, k : k + 1],
+            )
+
+        def deviation(r):
+            std[r] = work.tile([P, ROUND], F32, tag="std", bufs=3, name="std_tile")
+            nc.scalar.activation(out=std[r][:], in_=sq_sums[r][:], func=FUNC.Sqrt, bias=EPS, scale=1.0 / D**3)
+
+        def reciprocal_deviation(r):
+            rstd[r] = work.tile([P, ROUND], F32, tag="rstd", bufs=3, name="rstd_tile")
+            nc.vector.reciprocal(out=rstd[r][:], in_=std[r][:])
+
+        def centre_and_gain(r, k):
+            gained = work.tile([P, D], F32, tag="scaled", bufs=2 * ROUND)
+            scaled[r, k] = gained
+            nc.vector.scalar_tensor_tensor(
+                out=gained[:], in0=resid[r, k][:], scalar=neg_mean[r][:, k : k + 1], in1=g2_all[:],
+                op0=ALU.add, op1=ALU.mult,
+            )
+
+        def finish(r, k):
+            normed = work.tile([P, D], F32, tag="normed", bufs=ROUND + 2)
+            nc.vector.scalar_tensor_tensor(
+                out=normed[:], in0=scaled[r, k][:], scalar=rstd[r][:, k : k + 1], in1=beta2_all[:],
+                op0=ALU.mult, op1=ALU.add,
+            )
+            nc.sync.dma_start(out=out_rows[:, r * ROUND + k, :], in_=normed[:])
 
         def live(r):
             return 0 <= r < ROUNDS
 
-        transpose_h(0)
-        quantise_h(0)
-        prepare_vectors()
-        residual_and_bias(0)
-        for step in range(-1, ROUNDS + 1):
-            if live(step + 1):
-                first_matmul(step + 1)
-            if live(step + 2):
-                transpose_h(step + 2)
-            if live(step):
-                second_matmul(step)
-            if live(step + 2):
-                residual_and_bias(step + 2)
-            if live(step + 1):
-                hidden_to_words(step + 1)
-            if live(step + 2):
-                quantise_h(step + 2)
-            if live(step):
-                centre_and_gain(step)
-            if live(step + 1):
-                quantise_hidden(step + 1)
-            if live(step - 1):
-                finish(step - 1)
+        chunks = [(g, t) for g in range(F_PASSES) for t in range(4)]
+        tiles = range(ROUND)
+
+        def fill():
+            for half in range(2):
+                transpose_h(0, half)
+            reorder_w1()
+            quantise_h(0)
+            spread_vectors()
+            for k in tiles:
+                residual_and_bias(0, k, "gpsimd")
+            for j, (g, t) in enumerate(chunks):
+                hidden_product(0, g, t)
+                hidden_copy(0, g, t, "vector" if t % 2 else "scalar")
+                if j in (1, 2):
+                    transpose_h(1, j - 1)
+                if j in (3, 4):
+                    residual_and_bias(1, j - 3, "vector")
+                if j == 4:
+                    quantise_h(1)
+                if j == 5:
+                    hidden_to_words(0, 0, "vector")
+            for half in range(2):
+                transpose_h(2, half)
+            hidden_to_words(0, 1, "vector")
+            for j, (g, t) in enumerate(chunks):
+                hidden_product(1, g, t)
+                hidden_copy(1, g, t, "vector" if t % 2 else "scalar")
+                if j == 1:
+                    quantise_hidden(0, 0)
+                if j == 3:
+                    quantise_h(2)
+                    quantise_hidden(0, 1)
+                    hidden_to_words(1, 0, "gpsimd")
+            for k in (2, 3):
+                residual_and_bias(1, k, "vector")
+            for half in range(2):
+                transpose_h(3, half)
+            hidden_to_words(1, 1, "gpsimd")
+            for k in tiles:
+                residual_and_bias(2, k, "scalar")
+
+        def step(s):
+            for k in tiles:
+                add_up(s, k)
+            if live(s + 1):
+                quantise_hidden(s + 1, 0)
+            mean(s)
+            if live(s + 1):
+                quantise_hidden(s + 1, 1)
+            if live(s + 3):
+                quantise_h(s + 3)
+            for j, (g, t) in enumerate(chunks):
+                if live(s + 2):
+                    hidden_product(s + 2, g, t)
+                if j < ROUND:
+                    square(s, j)
+                if j == ROUND:
+                    deviation(s)
+                if live(s + 2) and j < 7:
+                    hidden_copy(s + 2, g, t, "scalar")
+                if j == 3:
+                    if live(s + 2):
+                        hidden_to_words(s + 2, 0, "gpsimd")
+                    for k in tiles:
+                        centre_and_gain(s, k)
+                if live(s + 4) and j in (5, 6):
+                    transpose_h(s + 4, j - 5)
+            reciprocal_deviation(s)
+            for k in tiles:
+                finish(s, k)
+                if k == 2 and live(s + 2):
+                    hidden_copy(s + 2, 1, 3, "vector")
+                    hidden_to_words(s + 2, 1, "gpsimd")
+            if live(s + 3):
+                for k in tiles:
+                    residual_and_bias(s + 3, k, "scalar")
+
+        with tc.manual_schedule(engines={mybir.EngineType.PE, mybir.EngineType.Activation, mybir.EngineType.DVE, mybir.EngineType.Pool}):
+            fill()
+            for s in range(ROUNDS):
+                step(s)

@@ -37,7 +37,7 @@ def tile_ffnn_encoder_pc_t_kernel(
     with ExitStack() as ctx:
         const = ctx.enter_context(tc.tile_pool(name="const", bufs=1))
         work = ctx.enter_context(tc.tile_pool(name="work", bufs=2))
-        psum = ctx.enter_context(tc.psum_pool(name="psum", bufs=6))
+        psum = ctx.enter_context(tc.psum_pool(name="psum", bufs=7))
         psum_const = ctx.enter_context(tc.psum_pool(name="psum_const", bufs=1))
 
         h_sb = const.tile([P, TILES, D], BF16)
@@ -51,8 +51,10 @@ def tile_ffnn_encoder_pc_t_kernel(
         b1_col = const.tile([P, F_PASSES, 4], F32)
         vec_rows = const.tile([P, 3 * D], BF16)
         b2_all = const.tile([P, D], F32)
-        g2_all = psum_const.tile([P, D], F32, tag="g2_all")
-        beta2_all = psum_const.tile([P, D], F32, tag="beta2_all")
+        beta2_sb = const.tile([P, D], F32)
+        affine = psum_const.tile([P, 2 * D], BF16, tag="affine")
+        g2_all = affine[:, 0:D]
+        beta2_all = affine[:, D : 2 * D]
         ones = const.tile([P, P], BF16)
         ident = const.tile([P, P], F32)
         ident_bf = const.tile([P, P], BF16)
@@ -117,10 +119,11 @@ def tile_ffnn_encoder_pc_t_kernel(
 
         def spread_vectors():
             bank = psum.tile([P, D], F32, tag="bank")
-            for i, spread in enumerate((bank, g2_all, beta2_all)):
+            for i, spread in enumerate((bank[:], g2_all, beta2_all)):
                 cols = slice(i * D, (i + 1) * D)
-                nc.tensor.matmul(out=spread[:], lhsT=ones[:], rhs=vec_rows[:, cols], start=True, stop=True)
+                nc.tensor.matmul(out=spread, lhsT=ones[:], rhs=vec_rows[:, cols], start=True, stop=True)
             nc.vector.tensor_copy(out=b2_all[:], in_=bank[:])
+            nc.scalar.copy(out=beta2_sb[:], in_=beta2_all)
 
         h_grouped = {}
         hq = {}
@@ -276,16 +279,23 @@ def tile_ffnn_encoder_pc_t_kernel(
             gained = work.tile([P, D], F32, tag="scaled", bufs=2 * ROUND)
             scaled[r, k] = gained
             nc.vector.scalar_tensor_tensor(
-                out=gained[:], in0=resid[r, k][:], scalar=neg_mean[r][:, k : k + 1], in1=g2_all[:],
+                out=gained[:], in0=resid[r, k][:], scalar=neg_mean[r][:, k : k + 1], in1=g2_all,
                 op0=ALU.add, op1=ALU.mult,
             )
 
         def finish(r, k):
             normed = work.tile([P, D], F32, tag="normed", bufs=ROUND + 2)
             nc.vector.scalar_tensor_tensor(
-                out=normed[:], in0=scaled[r, k][:], scalar=rstd[r][:, k : k + 1], in1=beta2_all[:],
+                out=normed[:], in0=scaled[r, k][:], scalar=rstd[r][:, k : k + 1], in1=beta2_all,
                 op0=ALU.mult, op1=ALU.add,
             )
+            nc.sync.dma_start(out=out_rows[:, r * ROUND + k, :], in_=normed[:])
+
+        def finish_elsewhere(r, k):
+            unit = work.tile([P, D], F32, tag="unit", bufs=3)
+            nc.scalar.activation(out=unit[:], in_=scaled[r, k][:], func=FUNC.Copy, scale=rstd[r][:, k : k + 1])
+            normed = work.tile([P, D], F32, tag="normed", bufs=ROUND + 2)
+            nc.gpsimd.tensor_tensor(out=normed[:], in0=unit[:], in1=beta2_sb[:], op=ALU.add)
             nc.sync.dma_start(out=out_rows[:, r * ROUND + k, :], in_=normed[:])
 
         def live(r):
@@ -307,12 +317,12 @@ def tile_ffnn_encoder_pc_t_kernel(
                 hidden_copy(0, g, t, "vector" if t % 2 else "scalar")
                 if j in (1, 2):
                     transpose_h(1, j - 1)
-                if j in (3, 4):
-                    residual_and_bias(1, j - 3, "vector")
                 if j == 4:
                     quantise_h(1)
                 if j == 5:
                     hidden_to_words(0, 0, "vector")
+            for k in (0, 1, 2):
+                residual_and_bias(1, k, "gpsimd")
             for half in range(2):
                 transpose_h(2, half)
             hidden_to_words(0, 1, "vector")
@@ -325,8 +335,7 @@ def tile_ffnn_encoder_pc_t_kernel(
                     quantise_h(2)
                     quantise_hidden(0, 1)
                     hidden_to_words(1, 0, "gpsimd")
-            for k in (2, 3):
-                residual_and_bias(1, k, "vector")
+            residual_and_bias(1, 3, "vector")
             for half in range(2):
                 transpose_h(3, half)
             hidden_to_words(1, 1, "gpsimd")
@@ -336,10 +345,18 @@ def tile_ffnn_encoder_pc_t_kernel(
         def step(s):
             for k in tiles:
                 add_up(s, k)
+            if s == ROUNDS - 1:
+                finish_elsewhere(s - 1, 2)
+                finish_elsewhere(s - 1, 3)
+            if 0 < s < ROUNDS - 1:
+                finish(s - 1, 2)
+            mean(s)
+            if 0 < s < ROUNDS - 1:
+                finish(s - 1, 3)
+            centre_and_gain(s, 0)
+            centre_and_gain(s, 1)
             if live(s + 1):
                 quantise_hidden(s + 1, 0)
-            mean(s)
-            if live(s + 1):
                 quantise_hidden(s + 1, 1)
             if live(s + 3):
                 quantise_h(s + 3)
@@ -348,28 +365,33 @@ def tile_ffnn_encoder_pc_t_kernel(
                     hidden_product(s + 2, g, t)
                 if j < ROUND:
                     square(s, j)
-                if j == ROUND:
+                if j == ROUND - 1:
                     deviation(s)
-                if live(s + 2) and j < 7:
+                if live(s + 2):
                     hidden_copy(s + 2, g, t, "scalar")
-                if j == 3:
-                    if live(s + 2):
-                        hidden_to_words(s + 2, 0, "gpsimd")
-                    for k in tiles:
-                        centre_and_gain(s, k)
+                if j == 3 and live(s + 2):
+                    hidden_to_words(s + 2, 0, "gpsimd")
                 if live(s + 4) and j in (5, 6):
                     transpose_h(s + 4, j - 5)
+            centre_and_gain(s, 2)
             reciprocal_deviation(s)
-            for k in tiles:
-                finish(s, k)
-                if k == 2 and live(s + 2):
-                    hidden_copy(s + 2, 1, 3, "vector")
-                    hidden_to_words(s + 2, 1, "gpsimd")
+            centre_and_gain(s, 3)
+            if s == ROUNDS - 1:
+                finish_elsewhere(s, 0)
+            else:
+                finish(s, 0)
+            finish(s, 1)
+            if live(s + 2):
+                hidden_to_words(s + 2, 1, "gpsimd")
             if live(s + 3):
                 for k in tiles:
-                    residual_and_bias(s + 3, k, "scalar")
+                    residual_and_bias(s + 3, k, "gpsimd" if k == 0 else "scalar")
 
-        with tc.manual_schedule(engines={mybir.EngineType.PE, mybir.EngineType.Activation, mybir.EngineType.DVE, mybir.EngineType.Pool}):
+        with tc.manual_schedule(
+            engines={mybir.EngineType.PE, mybir.EngineType.Activation, mybir.EngineType.DVE, mybir.EngineType.Pool}
+        ):
             fill()
             for s in range(ROUNDS):
                 step(s)
+            for k in (2, 3):
+                finish(ROUNDS - 1, k)

@@ -219,7 +219,7 @@ def tile_ffnn_encoder_pc_t_kernel(
 
         def residual_and_bias(r, k, engine):
             h_tile = h_sb[:, r * ROUND + k, :]
-            both = work.tile([P, D], F32, tag="hb", bufs=4 * ROUND)
+            both = work.tile([P, D], F32, tag="hb", bufs=3 * ROUND)
             hb[r, k] = both
             if engine == "gpsimd":
                 nc.gpsimd.tensor_tensor(out=both[:], in0=h_tile, in1=b2_all[:], op=ALU.add)
@@ -312,52 +312,50 @@ def tile_ffnn_encoder_pc_t_kernel(
             spread_vectors()
             for k in tiles:
                 residual_and_bias(0, k, "gpsimd")
+            residual_and_bias(1, 0, "gpsimd")
             for j, (g, t) in enumerate(chunks):
                 hidden_product(0, g, t)
                 hidden_copy(0, g, t, "vector" if t % 2 else "scalar")
                 if j in (1, 2):
                     transpose_h(1, j - 1)
-                if j == 4:
+                if j == 3:
                     quantise_h(1)
                 if j == 5:
                     hidden_to_words(0, 0, "vector")
-            for k in (0, 1, 2):
-                residual_and_bias(1, k, "gpsimd")
             for half in range(2):
                 transpose_h(2, half)
             hidden_to_words(0, 1, "vector")
-            for j, (g, t) in enumerate(chunks):
+            for g in range(F_PASSES):
+                quantise_hidden(0, g)
+            for g, t in chunks:
                 hidden_product(1, g, t)
-                hidden_copy(1, g, t, "vector" if t % 2 else "scalar")
-                if j == 1:
-                    quantise_hidden(0, 0)
-                if j == 3:
-                    quantise_h(2)
-                    quantise_hidden(0, 1)
-                    hidden_to_words(1, 0, "gpsimd")
-            residual_and_bias(1, 3, "vector")
+                hidden_copy(1, g, t, "scalar")
+                if t == 3:
+                    hidden_to_words(1, g, "gpsimd")
+            residual_and_bias(2, 0, "gpsimd")
+            quantise_h(2)
             for half in range(2):
                 transpose_h(3, half)
-            hidden_to_words(1, 1, "gpsimd")
-            for k in tiles:
-                residual_and_bias(2, k, "scalar")
 
         def step(s):
+            last = s == ROUNDS - 1
             for k in tiles:
                 add_up(s, k)
-            if s == ROUNDS - 1:
-                finish_elsewhere(s - 1, 2)
-                finish_elsewhere(s - 1, 3)
-            if 0 < s < ROUNDS - 1:
+            if s >= ROUNDS - 2:
+                for k in (2, 3):
+                    finish_elsewhere(s - 1, k)
+            if last:
+                finish(s - 1, 1)
+            elif 0 < s < ROUNDS - 2:
                 finish(s - 1, 2)
             mean(s)
-            if 0 < s < ROUNDS - 1:
+            if 0 < s < ROUNDS - 2:
                 finish(s - 1, 3)
             centre_and_gain(s, 0)
             centre_and_gain(s, 1)
             if live(s + 1):
-                quantise_hidden(s + 1, 0)
-                quantise_hidden(s + 1, 1)
+                for g in range(F_PASSES):
+                    quantise_hidden(s + 1, g)
             if live(s + 3):
                 quantise_h(s + 3)
             for j, (g, t) in enumerate(chunks):
@@ -369,23 +367,21 @@ def tile_ffnn_encoder_pc_t_kernel(
                     deviation(s)
                 if live(s + 2):
                     hidden_copy(s + 2, g, t, "scalar")
-                if j == 3 and live(s + 2):
-                    hidden_to_words(s + 2, 0, "gpsimd")
+                if t == 3 and live(s + 2):
+                    hidden_to_words(s + 2, g, "gpsimd")
                 if live(s + 4) and j in (5, 6):
                     transpose_h(s + 4, j - 5)
             centre_and_gain(s, 2)
             reciprocal_deviation(s)
             centre_and_gain(s, 3)
-            if s == ROUNDS - 1:
-                finish_elsewhere(s, 0)
-            else:
-                finish(s, 0)
-            finish(s, 1)
-            if live(s + 2):
-                hidden_to_words(s + 2, 1, "gpsimd")
+            finish(s, 0)
+            if s != ROUNDS - 2:
+                finish(s, 1)
             if live(s + 3):
-                for k in tiles:
-                    residual_and_bias(s + 3, k, "gpsimd" if k == 0 else "scalar")
+                residual_and_bias(s + 3, 0, "gpsimd")
+            if live(s + 1):
+                for k in (1, 2, 3):
+                    residual_and_bias(s + 1, k, "scalar")
 
         with tc.manual_schedule(
             engines={mybir.EngineType.PE, mybir.EngineType.Activation, mybir.EngineType.DVE, mybir.EngineType.Pool}

@@ -68,7 +68,7 @@ def tile_ffnn_encoder_pc_t_kernel(
         nc.vector.memset(one_col[:], 1.0)
         make_identity(nc, ident[:])
         make_identity(nc, ident_bf[:])
-        nc.scalar.activation(out=sqrt_warm[:], in_=one_col[:], func=FUNC.Sqrt)
+        nc.scalar.activation(out=sqrt_warm[:], in_=one_col[:], func=FUNC.Abs_reciprocal_sqrt)
 
         def load_h(r):
             tiles = slice(r * ROUND, (r + 1) * ROUND)
@@ -136,7 +136,6 @@ def tile_ffnn_encoder_pc_t_kernel(
         sums = {}
         neg_mean = {}
         sq_sums = {}
-        std = {}
         rstd = {}
         scaled = {}
 
@@ -256,7 +255,11 @@ def tile_ffnn_encoder_pc_t_kernel(
 
         def mean(r):
             neg_mean[r] = work.tile([P, ROUND], F32, tag="neg_mean", bufs=3, name="neg_mean_tile")
-            nc.vector.tensor_scalar_mul(out=neg_mean[r][:], in0=sums[r][:], scalar1=-1.0 / D)
+            total = work.tile([P, 1], F32, tag="total", bufs=3)
+            nc.vector.tensor_scalar(
+                out=neg_mean[r][:], in0=sums[r][:], scalar1=-1.0 / D, scalar2=None,
+                op0=ALU.mult, op1=ALU.add, accum_out=total[:],
+            )
 
         def square(r, k):
             if k == 0:
@@ -267,13 +270,11 @@ def tile_ffnn_encoder_pc_t_kernel(
                 bias=sums[r][:, k : k + 1], scale=-float(D), accum_out=sq_sums[r][:, k : k + 1],
             )
 
-        def deviation(r):
-            std[r] = work.tile([P, ROUND], F32, tag="std", bufs=3, name="std_tile")
-            nc.scalar.activation(out=std[r][:], in_=sq_sums[r][:], func=FUNC.Sqrt, bias=EPS, scale=1.0 / D**3)
-
         def reciprocal_deviation(r):
             rstd[r] = work.tile([P, ROUND], F32, tag="rstd", bufs=3, name="rstd_tile")
-            nc.vector.reciprocal(out=rstd[r][:], in_=std[r][:])
+            nc.scalar.activation(
+                out=rstd[r][:], in_=sq_sums[r][:], func=FUNC.Abs_reciprocal_sqrt, bias=EPS, scale=1.0 / D**3
+            )
 
         def centre_and_gain(r, k):
             gained = work.tile([P, D], F32, tag="scaled", bufs=2 * ROUND)
@@ -364,7 +365,7 @@ def tile_ffnn_encoder_pc_t_kernel(
                 if j < ROUND:
                     square(s, j)
                 if j == ROUND - 1:
-                    deviation(s)
+                    reciprocal_deviation(s)
                 if live(s + 2):
                     hidden_copy(s + 2, g, t, "scalar")
                 if t == 3 and live(s + 2):
@@ -372,7 +373,6 @@ def tile_ffnn_encoder_pc_t_kernel(
                 if live(s + 4) and j in (5, 6):
                     transpose_h(s + 4, j - 5)
             centre_and_gain(s, 2)
-            reciprocal_deviation(s)
             centre_and_gain(s, 3)
             finish(s, 0)
             if s != ROUNDS - 2:

@@ -90,6 +90,7 @@ def tile_ffnn_encoder_pc_t_kernel(
                 out=vec_rows[0:1, i * D : (i + 1) * D], in_=vec.rearrange("(o n) -> o n", o=1)
             )
         load_h(1)
+        load_h(2)
         for g in range(F_PASSES):
             for row in range(4):
                 nc.sync.dma_start(
@@ -101,7 +102,7 @@ def tile_ffnn_encoder_pc_t_kernel(
                 out=w2_codes[:, g, :].bitcast(I32),
                 in_=W2_words[g].rearrange("p n t -> p (n t)").bitcast(I32),
             )
-        for r in range(2, ROUNDS):
+        for r in range(3, ROUNDS):
             load_h(r)
 
         def reorder_w1():
@@ -125,6 +126,7 @@ def tile_ffnn_encoder_pc_t_kernel(
             nc.vector.tensor_copy(out=b2_all[:], in_=bank[:])
             nc.scalar.copy(out=beta2_sb[:], in_=beta2_all)
 
+        h_in_banks = {}
         h_grouped = {}
         hq = {}
         products = {}
@@ -147,7 +149,12 @@ def tile_ffnn_encoder_pc_t_kernel(
                 words = h_sb[:, r * ROUND + half * 2 + j, :].bitcast(F32)
                 for u in range(2):
                     nc.tensor.transpose(hT[:, j, u, :], words[:, u : D // 2 : 2], ident[:])
-            nc.scalar.copy(
+            h_in_banks[r, half] = hT
+
+        def copy_h(r, half, engine):
+            hT = h_in_banks[r, half]
+            copy = nc.vector.tensor_copy if engine == "vector" else nc.scalar.copy
+            copy(
                 out=h_grouped[r][:, half * 2 * P * 4 : (half + 1) * 2 * P * 4]
                 .bitcast(F32)
                 .rearrange("p (j k u) -> p j k u", j=2, u=2),
@@ -308,23 +315,28 @@ def tile_ffnn_encoder_pc_t_kernel(
         def fill():
             for half in range(2):
                 transpose_h(0, half)
+                copy_h(0, half, "scalar")
             reorder_w1()
             quantise_h(0)
             spread_vectors()
-            for k in tiles:
+            for k in (1, 2, 3):
                 residual_and_bias(0, k, "gpsimd")
             residual_and_bias(1, 0, "gpsimd")
             for j, (g, t) in enumerate(chunks):
                 hidden_product(0, g, t)
                 hidden_copy(0, g, t, "vector" if t % 2 else "scalar")
+                if j == 1:
+                    residual_and_bias(0, 0, "vector")
                 if j in (1, 2):
                     transpose_h(1, j - 1)
+                    copy_h(1, j - 1, "scalar")
                 if j == 3:
                     quantise_h(1)
                 if j == 5:
                     hidden_to_words(0, 0, "vector")
             for half in range(2):
                 transpose_h(2, half)
+                copy_h(2, half, "scalar")
             hidden_to_words(0, 1, "vector")
             for g in range(F_PASSES):
                 quantise_hidden(0, g)
@@ -337,6 +349,7 @@ def tile_ffnn_encoder_pc_t_kernel(
             quantise_h(2)
             for half in range(2):
                 transpose_h(3, half)
+                copy_h(3, half, "scalar")
 
         def step(s):
             last = s == ROUNDS - 1
@@ -372,9 +385,16 @@ def tile_ffnn_encoder_pc_t_kernel(
                     hidden_to_words(s + 2, g, "gpsimd")
                 if live(s + 4) and j in (5, 6):
                     transpose_h(s + 4, j - 5)
+                    if j == 5:
+                        copy_h(s + 4, 0, "scalar")
+            if last:
+                finish_elsewhere(s, 0)
             centre_and_gain(s, 2)
             centre_and_gain(s, 3)
-            finish(s, 0)
+            if not last:
+                finish(s, 0)
+            if live(s + 4):
+                copy_h(s + 4, 1, "vector")
             if s != ROUNDS - 2:
                 finish(s, 1)
             if live(s + 3):

from contextlib import ExitStack

import concourse.mybir as mybir
from concourse.masks import make_identity

F32 = mybir.dt.float32
BF16 = mybir.dt.bfloat16
I32 = mybir.dt.int32
U32 = mybir.dt.uint32
U8 = mybir.dt.uint8
FP8X4 = mybir.dt.float8_e4m3fn_x4
ALU = mybir.AluOpType
FUNC = mybir.ActivationFunctionType

P = 128
TOKENS = 4096
D = 512
F = 1024
K_PASS = 512
F_PASSES = F // K_PASS
TILES = TOKENS // P
ROUND = 4
ROUND_TOKENS = ROUND * P
ROUNDS = TILES // ROUND
EPS = 1e-3

FLOPS = 2 * TOKENS * D * F * 2


def tile_ffnn_encoder_pc_t_kernel(
    tc, h_attn, W1_words, W1_scales, b1, W2_words, W2_scales, b2, g2, beta2, out
):
    nc = tc.nc
    h_rows = h_attn.flatten_outer_dims().rearrange("(p n) d -> p n d", p=P)
    out_rows = out.flatten_outer_dims().rearrange("(p n) d -> p n d", p=P)

    with ExitStack() as ctx:
        const = ctx.enter_context(tc.tile_pool(name="const", bufs=1))
        work = ctx.enter_context(tc.tile_pool(name="work", bufs=2))
        psum = ctx.enter_context(tc.psum_pool(name="psum", bufs=7))
        psum_const = ctx.enter_context(tc.psum_pool(name="psum_const", bufs=1))

        h_sb = const.tile([P, TILES, D], BF16)
        w1_codes_raw = const.tile([P, F], U32, align_bytes=64)
        w1_plane_raw = const.tile([P, F], U8, align_bytes=64)
        w1_codes = const.tile([P, F_PASSES, 4, P], U32, align_bytes=64)
        w1_plane = const.tile([P, F_PASSES, 4, P], U8, align_bytes=64)
        w2_codes = const.tile([P, F_PASSES, D], U32, align_bytes=64)
        w2_plane = const.tile([P, F_PASSES, D], U8, align_bytes=64)
        b1_bf = const.tile([P, F_PASSES, 4], BF16)
        b1_col = const.tile([P, F_PASSES, 4], F32)
        vec_rows = const.tile([P, 3 * D], BF16)
        b2_all = const.tile([P, D], F32)
        beta2_sb = const.tile([P, D], F32)
        affine = psum_const.tile([P, 2 * D], BF16, tag="affine")
        g2_all = affine[:, 0:D]
        beta2_all = affine[:, D : 2 * D]
        ones = const.tile([P, P], BF16)
        ident = const.tile([P, P], F32)
        ident_bf = const.tile([P, P], BF16)
        one_col = const.tile([P, 1], F32)
        sqrt_warm = const.tile([P, 1], F32)

        nc.vector.memset(w1_plane_raw[:].bitcast(I32), 0)
        nc.vector.memset(vec_rows[:].bitcast(I32), 0)
        nc.vector.memset(w2_plane[:].bitcast(I32), 0)
        nc.vector.memset(ones[:], 1.0)
        nc.vector.memset(one_col[:], 1.0)
        make_identity(nc, ident[:])
        make_identity(nc, ident_bf[:])
        nc.scalar.activation(out=sqrt_warm[:], in_=one_col[:], func=FUNC.Abs_reciprocal_sqrt)

        def load_h(r):
            tiles = slice(r * ROUND, (r + 1) * ROUND)
            nc.sync.dma_start(out=h_sb[:, tiles, :], in_=h_rows[:, tiles, :])

        load_h(0)
        for row in range(4):
            nc.sync.dma_start(
                out=w1_plane_raw[row:P:32, :].bitcast(I32),
                in_=W1_scales[0, row:16:4, :].bitcast(I32),
            )
        nc.sync.dma_start(
            out=w1_codes_raw[:].bitcast(I32),
            in_=W1_words[0].rearrange("p n t -> p (n t)").bitcast(I32),
        )
        nc.sync.dma_start(out=b1_bf[:], in_=b1.rearrange("(g p t) -> p g t", p=P, t=4))
        for i, vec in enumerate((b2, g2, beta2)):
            nc.sync.dma_start(
                out=vec_rows[0:1, i * D : (i + 1) * D], in_=vec.rearrange("(o n) -> o n", o=1)
            )
        load_h(1)
        load_h(2)
        for g in range(F_PASSES):
            for row in range(4):
                nc.sync.dma_start(
                    out=w2_plane[row:P:32, g, :].bitcast(I32),
                    in_=W2_scales[g, row:16:4, :].bitcast(I32),
                )
        for g in range(F_PASSES):
            nc.sync.dma_start(
                out=w2_codes[:, g, :].bitcast(I32),
                in_=W2_words[g].rearrange("p n t -> p (n t)").bitcast(I32),
            )
        for r in range(3, ROUNDS):
            load_h(r)

        def reorder_w1():
            for g in range(F_PASSES):
                units = slice(g * K_PASS, (g + 1) * K_PASS)
                nc.vector.tensor_copy(
                    out=w1_plane[:, g, :, :],
                    in_=w1_plane_raw[:, units].rearrange("p (m t) -> p t m", t=4),
                )
                nc.vector.tensor_copy(
                    out=w1_codes[:, g, :, :].bitcast(I32),
                    in_=w1_codes_raw[:, units].bitcast(I32).rearrange("p (m t) -> p t m", t=4),
                )
            nc.vector.tensor_copy(out=b1_col[:], in_=b1_bf[:])

        def spread_vectors():
            bank = psum.tile([P, D], F32, tag="bank")
            for i, spread in enumerate((bank[:], g2_all, beta2_all)):
                cols = slice(i * D, (i + 1) * D)
                nc.tensor.matmul(out=spread, lhsT=ones[:], rhs=vec_rows[:, cols], start=True, stop=True)
            nc.vector.tensor_copy(out=b2_all[:], in_=bank[:])
            nc.scalar.copy(out=beta2_sb[:], in_=beta2_all)

        h_in_banks = {}
        h_grouped = {}
        hq = {}
        products = {}
        hid_by_unit = {}
        hid_grouped = {}
        hidq = {}
        hb = {}
        resid = {}
        sums = {}
        neg_mean = {}
        sq_sums = {}
        rstd = {}
        scaled = {}

        def transpose_h(r, half):
            if half == 0:
                h_grouped[r] = work.tile([P, ROUND_TOKENS * 4], BF16, align_bytes=64, tag="h_grouped", bufs=3, name="h_grouped_tile")
            hT = psum.tile([P, 2, 2, P], F32, tag="bank")
            for j in range(2):
                words = h_sb[:, r * ROUND + half * 2 + j, :].bitcast(F32)
                for u in range(2):
                    nc.tensor.transpose(hT[:, j, u, :], words[:, u : D // 2 : 2], ident[:])
            h_in_banks[r, half] = hT

        def copy_h(r, half, engine):
            hT = h_in_banks[r, half]
            copy = nc.vector.tensor_copy if engine == "vector" else nc.scalar.copy
            copy(
                out=h_grouped[r][:, half * 2 * P * 4 : (half + 1) * 2 * P * 4]
                .bitcast(F32)
                .rearrange("p (j k u) -> p j k u", j=2, u=2),
                in_=hT[:].rearrange("p j u k -> p j k u"),
            )

        def quantise_h(r):
            codes = work.tile([P, ROUND_TOKENS], U32, align_bytes=64, tag="hq_codes", bufs=3)
            plane = work.tile([P, ROUND_TOKENS], U8, align_bytes=64, tag="hq_plane", bufs=3)
            nc.vector.quantize_mx(out=codes[:].bitcast(FP8X4), scales=plane[:], in_=h_grouped[r][:])
            hq[r] = (codes, plane)

        def hidden_product(r, g, t):
            codes, plane = hq[r]
            acc1 = psum.tile([P, ROUND_TOKENS], F32, tag="bank")
            products[r, g, t] = acc1
            nc.tensor.matmul_mx(
                out=acc1[:],
                lhsT=w1_codes[:, g, t, :].bitcast(FP8X4),
                lhsT_scale=w1_plane[:, g, t, :],
                rhs=codes[:].bitcast(FP8X4),
                rhs_scale=plane[:],
                start=True,
                stop=True,
            )

        def hidden_copy(r, g, t, engine):
            if (r, g) not in hid_by_unit:
                hid_by_unit[r, g] = work.tile([P, 4, ROUND_TOKENS], BF16, tag="hid_by_unit", bufs=6, name="by_unit_tile")
            by_unit = hid_by_unit[r, g]
            acc1 = products[r, g, t]
            if engine == "vector":
                nc.vector.tensor_scalar(
                    out=by_unit[:, t, :], in0=acc1[:], scalar1=b1_col[:, g, t : t + 1], scalar2=0.0,
                    op0=ALU.add, op1=ALU.max,
                )
            else:
                nc.scalar.activation(
                    out=by_unit[:, t, :], in_=acc1[:], func=FUNC.Relu, bias=b1_col[:, g, t : t + 1], scale=1.0
                )

        def hidden_to_words(r, g, engine):
            grouped = work.tile([P, ROUND_TOKENS, 4], BF16, align_bytes=64, tag="hid_grouped", bufs=4)
            hid_grouped[r, g] = grouped
            if engine == "vector":
                nc.vector.tensor_copy(
                    out=grouped[:].rearrange("p (c i) t -> p c t i", i=4),
                    in_=hid_by_unit[r, g][:].rearrange("p t (c i) -> p c t i", i=4),
                )
            else:
                for half in range(2):
                    tokens = slice(half * ROUND_TOKENS // 2, (half + 1) * ROUND_TOKENS // 2)
                    nc.gpsimd.tensor_scalar(
                        out=grouped[:, tokens, :],
                        in0=hid_by_unit[r, g][:, :, tokens].rearrange("p t k -> p k t"),
                        scalar1=1.0, scalar2=0.0, op0=ALU.mult, op1=ALU.add,
                    )

        def quantise_hidden(r, g):
            codes = work.tile([P, ROUND_TOKENS], U32, align_bytes=64, tag="hid_codes", bufs=6)
            plane = work.tile([P, ROUND_TOKENS], U8, align_bytes=64, tag="hid_plane", bufs=6)
            hidq[r, g] = (codes, plane)
            nc.vector.quantize_mx(
                out=codes[:].bitcast(FP8X4),
                scales=plane[:],
                in_=hid_grouped[r, g][:].rearrange("p k t -> p (k t)"),
            )

        def residual_and_bias(r, k, engine):
            h_tile = h_sb[:, r * ROUND + k, :]
            both = work.tile([P, D], F32, tag="hb", bufs=3 * ROUND)
            hb[r, k] = both
            if engine == "gpsimd":
                nc.gpsimd.tensor_tensor(out=both[:], in0=h_tile, in1=b2_all[:], op=ALU.add)
            elif engine == "vector":
                nc.vector.tensor_tensor(out=both[:], in0=h_tile, in1=b2_all[:], op=ALU.add)
            else:
                bank = psum.tile([P, D], F32, tag="bank")
                nc.tensor.matmul(out=bank[:], lhsT=ident_bf[:], rhs=h_tile, start=True, stop=False)
                nc.tensor.matmul(out=bank[:], lhsT=ones[:], rhs=vec_rows[:, 0:D], start=False, stop=True)
                nc.scalar.copy(out=both[:], in_=bank[:])

        def add_up(r, k):
            if k == 0:
                sums[r] = work.tile([P, ROUND], F32, tag="sums", bufs=3, name="sums_tile")
            acc2 = psum.tile([P, D], F32, tag="bank")
            tokens = slice(k * P, (k + 1) * P)
            for g in range(F_PASSES):
                codes, plane = hidq[r, g]
                nc.tensor.matmul_mx(
                    out=acc2[:],
                    lhsT=codes[:, tokens].bitcast(FP8X4),
                    lhsT_scale=plane[:, tokens],
                    rhs=w2_codes[:, g, :].bitcast(FP8X4),
                    rhs_scale=w2_plane[:, g, :],
                    start=(g == 0),
                    stop=(g == F_PASSES - 1),
                )
            res = work.tile([P, D], F32, tag="resid", bufs=2 * ROUND)
            resid[r, k] = res
            nc.vector.scalar_tensor_tensor(
                out=res[:], in0=acc2[:], scalar=1.0, in1=hb[r, k][:],
                op0=ALU.mult, op1=ALU.add, accum_out=sums[r][:, k : k + 1],
            )

        def mean(r):
            neg_mean[r] = work.tile([P, ROUND], F32, tag="neg_mean", bufs=3, name="neg_mean_tile")
            total = work.tile([P, 1], F32, tag="total", bufs=3)
            nc.vector.tensor_scalar(
                out=neg_mean[r][:], in0=sums[r][:], scalar1=-1.0 / D, scalar2=None,
                op0=ALU.mult, op1=ALU.add, accum_out=total[:],
            )

        def square(r, k):
            if k == 0:
                sq_sums[r] = work.tile([P, ROUND], F32, tag="sq_sums", bufs=3, name="sq_sums_tile")
            squares = work.tile([P, D], BF16, tag="squares")
            nc.scalar.activation(
                out=squares[:], in_=resid[r, k][:], func=FUNC.Square,
                bias=sums[r][:, k : k + 1], scale=-float(D), accum_out=sq_sums[r][:, k : k + 1],
            )

        def reciprocal_deviation(r):
            rstd[r] = work.tile([P, ROUND], F32, tag="rstd", bufs=3, name="rstd_tile")
            nc.scalar.activation(
                out=rstd[r][:], in_=sq_sums[r][:], func=FUNC.Abs_reciprocal_sqrt, bias=EPS, scale=1.0 / D**3
            )

        def centre_and_gain(r, k):
            gained = work.tile([P, D], F32, tag="scaled", bufs=2 * ROUND)
            scaled[r, k] = gained
            nc.vector.scalar_tensor_tensor(
                out=gained[:], in0=resid[r, k][:], scalar=neg_mean[r][:, k : k + 1], in1=g2_all,
                op0=ALU.add, op1=ALU.mult,
            )

        def finish(r, k):
            normed = work.tile([P, D], F32, tag="normed", bufs=ROUND + 2)
            nc.vector.scalar_tensor_tensor(
                out=normed[:], in0=scaled[r, k][:], scalar=rstd[r][:, k : k + 1], in1=beta2_all,
                op0=ALU.mult, op1=ALU.add,
            )
            nc.sync.dma_start(out=out_rows[:, r * ROUND + k, :], in_=normed[:])

        def finish_elsewhere(r, k):
            unit = work.tile([P, D], F32, tag="unit", bufs=3)
            nc.scalar.activation(out=unit[:], in_=scaled[r, k][:], func=FUNC.Copy, scale=rstd[r][:, k : k + 1])
            normed = work.tile([P, D], F32, tag="normed", bufs=ROUND + 2)
            nc.gpsimd.tensor_tensor(out=normed[:], in0=unit[:], in1=beta2_sb[:], op=ALU.add)
            nc.sync.dma_start(out=out_rows[:, r * ROUND + k, :], in_=normed[:])

        def live(r):
            return 0 <= r < ROUNDS

        chunks = [(g, t) for g in range(F_PASSES) for t in range(4)]
        tiles = range(ROUND)

        def fill():
            for half in range(2):
                transpose_h(0, half)
                copy_h(0, half, "scalar")
            reorder_w1()
            quantise_h(0)
            spread_vectors()
            for k in (1, 2, 3):
                residual_and_bias(0, k, "gpsimd")
            residual_and_bias(1, 0, "gpsimd")
            for j, (g, t) in enumerate(chunks):
                hidden_product(0, g, t)
                hidden_copy(0, g, t, "vector" if t % 2 else "scalar")
                if j == 1:
                    residual_and_bias(0, 0, "vector")
                if j in (1, 2):
                    transpose_h(1, j - 1)
                    copy_h(1, j - 1, "scalar")
                if j == 3:
                    quantise_h(1)
                if j == 5:
                    hidden_to_words(0, 0, "vector")
            for half in range(2):
                transpose_h(2, half)
                copy_h(2, half, "scalar")
            hidden_to_words(0, 1, "vector")
            for g in range(F_PASSES):
                quantise_hidden(0, g)
            for g, t in chunks:
                hidden_product(1, g, t)
                hidden_copy(1, g, t, "scalar")
                if t == 3:
                    hidden_to_words(1, g, "gpsimd")
            residual_and_bias(2, 0, "gpsimd")
            quantise_h(2)
            for half in range(2):
                transpose_h(3, half)
                copy_h(3, half, "scalar")

        def step(s):
            last = s == ROUNDS - 1
            for k in tiles:
                add_up(s, k)
            if s >= ROUNDS - 2:
                for k in (2, 3):
                    finish_elsewhere(s - 1, k)
            if last:
                finish(s - 1, 1)
            elif 0 < s < ROUNDS - 2:
                finish(s - 1, 2)
            mean(s)
            if 0 < s < ROUNDS - 2:
                finish(s - 1, 3)
            centre_and_gain(s, 0)
            centre_and_gain(s, 1)
            if live(s + 1):
                for g in range(F_PASSES):
                    quantise_hidden(s + 1, g)
            if live(s + 3):
                quantise_h(s + 3)
            for j, (g, t) in enumerate(chunks):
                if live(s + 2):
                    hidden_product(s + 2, g, t)
                if j < ROUND:
                    square(s, j)
                if j == ROUND - 1:
                    reciprocal_deviation(s)
                if live(s + 2):
                    hidden_copy(s + 2, g, t, "scalar")
                if t == 3 and live(s + 2):
                    hidden_to_words(s + 2, g, "gpsimd")
                if live(s + 4) and j in (5, 6):
                    transpose_h(s + 4, j - 5)
                    if j == 5:
                        copy_h(s + 4, 0, "scalar")
            if last:
                finish_elsewhere(s, 0)
            centre_and_gain(s, 2)
            centre_and_gain(s, 3)
            if not last:
                finish(s, 0)
            if live(s + 4):
                copy_h(s + 4, 1, "vector")
            if s != ROUNDS - 2:
                finish(s, 1)
            if live(s + 3):
                residual_and_bias(s + 3, 0, "gpsimd")
            if live(s + 1):
                for k in (1, 2, 3):
                    residual_and_bias(s + 1, k, "scalar")

        with tc.manual_schedule(
            engines={mybir.EngineType.PE, mybir.EngineType.Activation, mybir.EngineType.DVE, mybir.EngineType.Pool}
        ):
            fill()
            for s in range(ROUNDS):
                step(s)
            for k in (2, 3):
                finish(ROUNDS - 1, k)
